import numpy as np
import ml_dtypes


def mxq(x, axis, fmt="e4m3"):
    dtype, down = {"e4m3": (ml_dtypes.float8_e4m3fn, 7), "e5m2": (ml_dtypes.float8_e5m2, 14)}[fmt]
    v = np.moveaxis(np.asarray(x, np.float32).astype(ml_dtypes.bfloat16).astype(np.float64), axis, -1)
    blocks = v.reshape(v.shape[:-1] + (-1, 32))
    amax = np.abs(blocks).max(-1, keepdims=True)
    byte = np.maximum(np.where(amax > 0, np.frexp(amax)[1] - 1 + 127, 0) - down, 1)
    scale = np.exp2(byte - 127.0)
    codes = (blocks / scale).astype(np.float32).astype(dtype).astype(np.float64)
    return np.moveaxis((codes * scale).reshape(v.shape), -1, axis)


WIDE = False


def mx_kscale(k):
    if not WIDE:
        return np.ones(k)
    levels = np.array([10, -10, 5, -5, 0])
    if k % 512:
        return np.exp2(np.random.permutation(np.resize(levels, k // 32))).repeat(32)
    a = np.empty((k // 512, 16))
    for p in range(k // 512):
        a[p, :8] = np.random.permutation(np.resize(levels, 8))
        for g in range(8):
            far = levels[np.abs(levels - a[p, g]) >= 10]
            a[p, g + 8] = far[np.random.randint(len(far))]
    return np.exp2(a.ravel()).repeat(32)


BF16 = ml_dtypes.bfloat16


def bf(x):
    return np.asarray(x, np.float32).astype(BF16)


def f64(x):
    return np.asarray(x).astype(np.float64)


B, S, H, D, QB, DEPTH = 1, 1024, 4, 128, 512, 12
HP = H // 2
LAMBDA_INIT = 0.8 - 0.6 * np.exp(-0.3 * DEPTH)
NEG_INF = -1e30
EPS = 1e-5


def split_heads(x):
    x = x.reshape(x.shape[0], x.shape[1], x.shape[2] // 2, 2, x.shape[3])
    return x[..., 0, :], x[..., 1, :]


def causal_attn(q, k, vq):
    rows = []
    for r0 in range(0, S, QB):
        r1 = r0 + QB
        s = (q[:, :, r0:r1] @ k[:, :, :r1].transpose(0, 1, 3, 2)) * (1.0 / np.sqrt(D))
        causal = np.arange(r0, r1)[:, None] >= np.arange(r1)[None, :]
        s = np.where(causal, s, NEG_INF)
        e = np.exp(s - s.max(-1, keepdims=True))
        rows.append((mxq(e, 3, "e4m3") @ vq[:, :, :r1]) / e.sum(-1, keepdims=True))
    return np.concatenate(rows, axis=2)


def setup_inputs():
    ls = 0.5 / D ** 0.25
    t = mx_kscale(S)
    qc = 0.25 * np.sqrt(D)
    q = np.random.standard_normal((B, S, H, D))
    k = np.random.standard_normal((B, S, H, D))
    v = np.random.standard_normal((B, S, H, D)) * 0.125
    q[..., 0] = qc
    k[..., 0] += (np.log(t) * np.sqrt(D) / qc)[None, :, None]
    v *= (t.mean() / t)[None, :, None, None]
    return {
        "q": bf(q),
        "k": bf(k),
        "v": bf(v),
        "lambda_q1": bf(np.random.standard_normal(D) * ls),
        "lambda_k1": bf(np.random.standard_normal(D) * ls),
        "lambda_q2": bf(np.random.standard_normal(D) * ls),
        "lambda_k2": bf(np.random.standard_normal(D) * ls),
        "subln_weight": bf(1.0 + 0.1 * np.random.standard_normal(2 * D)),
    }


def reference(q, k, v, lambda_q1, lambda_k1, lambda_q2, lambda_k2, subln_weight):
    q1, q2 = split_heads(f64(q))
    k1, k2 = split_heads(f64(k))
    v1, v2 = split_heads(f64(v))
    v12 = np.concatenate([v1, v2], axis=-1)
    vq = mxq(v12.transpose(0, 2, 1, 3), 2, "e4m3")
    attn1 = causal_attn(q1.transpose(0, 2, 1, 3), k1.transpose(0, 2, 1, 3), vq)
    attn2 = causal_attn(q2.transpose(0, 2, 1, 3), k2.transpose(0, 2, 1, 3), vq)
    lam1 = np.exp(np.sum(f64(lambda_q1) * f64(lambda_k1)))
    lam2 = np.exp(np.sum(f64(lambda_q2) * f64(lambda_k2)))
    lam = lam1 - lam2 + LAMBDA_INIT
    x = attn1 - lam * attn2
    var = np.mean(x * x, axis=-1, keepdims=True)
    xn = f64(subln_weight) * (x / np.sqrt(var + EPS))
    y = xn * (1.0 - LAMBDA_INIT)
    return y.transpose(0, 2, 1, 3).reshape(B, S, H, D)

@@ -1,0 +1,443 @@
+import math
+from contextlib import ExitStack
+
+import concourse.mybir as mybir
+from concourse.masks import make_identity
+
+BF16 = mybir.dt.bfloat16
+F32 = mybir.dt.float32
+U32 = mybir.dt.uint32
+U8 = mybir.dt.uint8
+FP8X4 = mybir.dt.float8_e4m3fn_x4
+ALU = mybir.AluOpType
+FUNC = mybir.ActivationFunctionType
+AXIS = mybir.AxisListType
+
+P = 128
+SEQ = 1024
+HEADS = 4
+DIM = 128
+ROW = HEADS * DIM
+PAIR_DIM = 2 * DIM
+PACK = 4
+K_PASS = P * PACK
+TILES_PER_PASS = K_PASS // P
+PASSES = SEQ // K_PASS
+Q_TILES = SEQ // P
+UNITS = Q_TILES * HEADS
+PAIR_UNITS = UNITS // 2
+
+SCALE = 1.0 / math.sqrt(DIM)
+LAMBDA_INIT = 0.8 - 0.6 * math.exp(-0.3 * 12)
+NEG_INF = -1e30
+EPS = 1e-5
+
+LAM_TICK = -3
+
+FLOPS = 2 * HEADS * (512 * 512 + 512 * 1024) * (DIM + PAIR_DIM)
+
+
+def passes_of(q_tile):
+    return q_tile // TILES_PER_PASS + 1
+
+
+def tile_refphi4flashdiffattention_pa_kernel(
+    tc, q, k, v, lambda_q1, lambda_k1, lambda_q2, lambda_k2, subln_weight, out
+):
+    nc = tc.nc
+
+    q_rows = q.rearrange("b (j p) h d -> p (b j) (h d)", p=P)
+    k_rows = k.rearrange("b (j p) h d -> p (b j) (h d)", p=P)
+    out_rows = out.rearrange("b (j p) h d -> p (b j) (h d)", p=P)
+    v_rows = v.rearrange("b (g p t) h d -> p (b g) (t h d)", p=P, t=PACK)
+
+    with ExitStack() as stack:
+        keep = stack.enter_context(tc.tile_pool(name="keep", bufs=1))
+        work = stack.enter_context(tc.tile_pool(name="work", bufs=4))
+        small = stack.enter_context(tc.tile_pool(name="small", bufs=6))
+        ps_s = stack.enter_context(tc.psum_pool(name="ps_s", bufs=4))
+        ps_t = stack.enter_context(tc.psum_pool(name="ps_t", bufs=2))
+        ps_o = stack.enter_context(tc.psum_pool(name="ps_o", bufs=2))
+
+        first_row = keep.tile([P, 4 * DIM + PAIR_DIM], BF16, name="first_row")
+        nc.vector.memset(first_row[:], 0.0)
+        for slot, vector in enumerate((lambda_q1, lambda_q2, lambda_k1, lambda_k2)):
+            nc.scalar.dma_start(
+                out=first_row[0:1, slot * DIM : (slot + 1) * DIM], in_=vector.unsqueeze(0)
+            )
+        nc.scalar.dma_start(out=first_row[0:1, 4 * DIM :], in_=subln_weight.unsqueeze(0))
+
+        q_sb = [keep.tile([P, ROW], BF16, name="q_sb%d" % j) for j in range(Q_TILES)]
+        k_sb = [keep.tile([P, ROW], BF16, name="k_sb%d" % j) for j in range(Q_TILES)]
+        v_raw = [keep.tile([P, PACK, ROW], BF16, name="v_raw%d" % g) for g in range(PASSES)]
+
+        def load_rows(j):
+            nc.sync.dma_start(out=k_sb[j][:], in_=k_rows[:, j, :])
+            nc.sync.dma_start(out=q_sb[j][:], in_=q_rows[:, j, :])
+
+        def load_values(g):
+            nc.sync.dma_start(out=v_raw[g][:].rearrange("p t c -> p (t c)"), in_=v_rows[:, g, :])
+
+        for j in range(Q_TILES):
+            load_rows(j)
+            if j % TILES_PER_PASS == 1:
+                load_values(j // TILES_PER_PASS)
+
+        ident_bf = keep.tile([P, P], BF16, name="ident_bf")
+        make_identity(nc, ident_bf[:])
+        mask_f32 = keep.tile([P, P], F32, name="mask_f32")
+        nc.gpsimd.memset(mask_f32[:], 0.0)
+        nc.gpsimd.affine_select(
+            out=mask_f32[:],
+            in_=mask_f32[:],
+            pattern=[[-1, P]],
+            compare_op=ALU.is_ge,
+            fill=NEG_INF,
+            base=0,
+            channel_multiplier=1,
+        )
+        mask_bf = keep.tile([P, P], BF16, name="mask_bf")
+        nc.vector.tensor_copy(out=mask_bf[:], in_=mask_f32[:])
+        ident_f32 = keep.tile([P, P], F32, name="ident_f32")
+        make_identity(nc, ident_f32[:])
+        minus_one = keep.tile([P, 2], F32, name="minus_one")
+        nc.gpsimd.memset(minus_one[:], -1.0)
+        minus_half = keep.tile([P, 1], F32, name="minus_half")
+        nc.gpsimd.memset(minus_half[:], -0.5)
+
+        e_tiles = []
+        for i in range(Q_TILES):
+            width = passes_of(i) * K_PASS
+            e_tile = keep.tile([P, HEADS, width], BF16, name="e_tile%d" % i)
+            seen = (i + 1) * P
+            if seen < width:
+                nc.vector.memset(e_tile[:, :, seen:width], 0.0)
+            e_tiles.append(e_tile)
+
+        ones = keep.tile([P, P], BF16, name="ones")
+        nc.vector.memset(ones[:], 1.0)
+        lam_in = keep.tile([P, 4, DIM], F32, name="lam_in")
+        products = keep.tile([P, 2, DIM], F32, name="products")
+        unread = keep.tile([P, 2, DIM], F32, name="unread")
+        dots = keep.tile([P, 2], F32, name="dots")
+        powers = keep.tile([P, 2], F32, name="powers")
+        difference = keep.tile([P, 1], F32, name="difference")
+        signs = keep.tile([P, 2], F32, name="signs")
+        nc.gpsimd.memset(signs[:, 0:1], 1.0)
+        gain = keep.tile([P, PAIR_DIM], F32, name="gain")
+        spread_banks = {}
+
+        def spread_vectors():
+            lam_bank = ps_s.tile([P, 4, DIM], F32, name="lam_bank", tag="s_bank")
+            nc.tensor.matmul(
+                out=lam_bank[:].rearrange("p s d -> p (s d)"),
+                lhsT=ones[:],
+                rhs=first_row[:, 0 : 4 * DIM],
+                start=True,
+                stop=True,
+            )
+            weight_bank = ps_s.tile([P, PAIR_DIM], F32, name="weight_bank", tag="s_bank")
+            nc.tensor.matmul(
+                out=weight_bank[:], lhsT=ones[:], rhs=first_row[:, 4 * DIM :], start=True, stop=True
+            )
+            spread_banks["lam"] = lam_bank
+            spread_banks["weight"] = weight_bank
+
+        def lam_products():
+            nc.scalar.copy(out=lam_in[:], in_=spread_banks["lam"][:])
+            nc.gpsimd.tensor_tensor(
+                out=products[:], in0=lam_in[:, 0:2, :], in1=lam_in[:, 2:4, :], op=ALU.mult
+            )
+
+        def scale_gain():
+            nc.scalar.mul(
+                out=gain[:],
+                in_=spread_banks["weight"][:],
+                mul=(1.0 - LAMBDA_INIT) * math.sqrt(PAIR_DIM),
+            )
+
+        def lam_dots():
+            for term in range(2):
+                nc.scalar.activation(
+                    out=unread[:, term, :],
+                    in_=products[:, term, :],
+                    func=FUNC.Copy,
+                    accum_out=dots[:, term : term + 1],
+                )
+
+        def lam_signs():
+            nc.scalar.activation(out=powers[:], in_=dots[:], func=FUNC.Exp)
+            nc.gpsimd.tensor_tensor(
+                out=difference[:], in0=powers[:, 1:2], in1=powers[:, 0:1], op=ALU.subtract
+            )
+            nc.gpsimd.tensor_scalar_add(out=signs[:, 1:2], in0=difference[:], scalar1=-LAMBDA_INIT)
+
+        v_grouped = [
+            keep.tile([P, ROW * PACK], BF16, name="v_grouped%d" % g, align_bytes=64)
+            for g in range(PASSES)
+        ]
+        v_codes = [
+            keep.tile([P, ROW], U32, name="v_codes%d" % g, align_bytes=64) for g in range(PASSES)
+        ]
+        v_scales = [
+            keep.tile([P, ROW], U8, name="v_scales%d" % g, align_bytes=64) for g in range(PASSES)
+        ]
+
+        def regroup_values(g):
+            nc.vector.tensor_copy(
+                out=v_grouped[g][:].rearrange("p (c i t) -> p c t i", i=4, t=PACK),
+                in_=v_raw[g][:].rearrange("p t (c i) -> p c t i", i=4),
+            )
+
+        def quantise_values(g):
+            nc.vector.quantize_mx(
+                out=v_codes[g][:].bitcast(FP8X4), scales=v_scales[g][:], in_=v_grouped[g][:]
+            )
+
+        q_turned = [keep.tile([P, HEADS, P], BF16, name="q_turned%d" % j) for j in range(Q_TILES)]
+        k_turned = [keep.tile([P, HEADS, K_PASS], BF16, name="k_turned%d" % g) for g in range(PASSES)]
+        rows_ps = {}
+
+        def turn_rows(j):
+            bank = ps_t.tile([P, 2, HEADS, P], BF16, name="rows_bank", tag="t")
+            for h in range(HEADS):
+                cols = slice(h * DIM, (h + 1) * DIM)
+                nc.tensor.transpose(bank[:, 0, h, :], q_sb[j][:, cols], ident_bf[:])
+                nc.tensor.transpose(bank[:, 1, h, :], k_sb[j][:, cols], ident_bf[:])
+            rows_ps[j] = bank
+
+        def copy_rows(j):
+            g, t = divmod(j, TILES_PER_PASS)
+            nc.vector.tensor_copy(out=q_turned[j][:], in_=rows_ps[j][:, 0, :, :])
+            nc.vector.tensor_copy(
+                out=k_turned[g][:, :, t * P : (t + 1) * P], in_=rows_ps[j][:, 1, :, :]
+            )
+
+        s_banks = {}
+        tops = {}
+        shifts = {}
+        row_sums = {}
+        e_banks = {}
+        e_grouped = {}
+        e_codes = {}
+        e_scales = {}
+        o_banks = {}
+
+        def scores(n):
+            i, h = divmod(n, HEADS)
+            banks = []
+            for g in range(passes_of(i)):
+                width = min(i + 1 - g * TILES_PER_PASS, TILES_PER_PASS) * P
+                holds_diagonal = g == passes_of(i) - 1
+                bank = ps_s.tile([P, K_PASS], F32, name="s_bank")
+                nc.tensor.matmul(
+                    out=bank[:, 0:width],
+                    lhsT=q_turned[i][:, h, :],
+                    rhs=k_turned[g][:, h, 0:width],
+                    start=True,
+                    stop=not holds_diagonal,
+                )
+                if holds_diagonal:
+                    nc.tensor.matmul(
+                        out=bank[:, width - P : width],
+                        lhsT=ident_bf[:],
+                        rhs=mask_bf[:],
+                        start=False,
+                        stop=True,
+                    )
+                banks.append((bank, width))
+            s_banks[n] = banks
+
+        def row_tops(n):
+            top = small.tile([P, PASSES], F32, name="top")
+            for g, (bank, width) in enumerate(s_banks[n]):
+                nc.vector.tensor_reduce(
+                    out=top[:, g : g + 1], in_=bank[:, 0:width], axis=AXIS.X, op=ALU.max
+                )
+            tops[n] = top
+
+        def shift(n):
+            bias = small.tile([P, 1], F32, name="bias")
+            if len(s_banks[n]) == 2:
+                nc.vector.tensor_scalar(
+                    out=bias[:],
+                    in0=tops[n][:, 0:1],
+                    scalar1=tops[n][:, 1:2],
+                    scalar2=-SCALE,
+                    op0=ALU.max,
+                    op1=ALU.mult,
+                )
+            else:
+                nc.vector.tensor_scalar_mul(out=bias[:], in0=tops[n][:, 0:1], scalar1=-SCALE)
+            shifts[n] = bias
+
+        def exponent(n):
+            i, h = divmod(n, HEADS)
+            m, half = divmod(n, 2)
+            if half == 0:
+                row_sums[m] = small.tile([P, 2, passes_of(i)], F32, name="row_sum")
+            for g, (bank, width) in enumerate(s_banks[n]):
+                nc.scalar.activation(
+                    out=e_tiles[i][:, h, g * K_PASS : g * K_PASS + width],
+                    in_=bank[:, 0:width],
+                    func=FUNC.Exp,
+                    bias=shifts[n][:, 0:1],
+                    scale=SCALE,
+                    accum_out=row_sums[m][:, half, g : g + 1],
+                )
+
+        def turn(n):
+            i, h = divmod(n, HEADS)
+            words = e_tiles[i][:, h, :].bitcast(F32)
+            bank = ps_t.tile([P, passes_of(i), 2, P], F32, name="e_bank", tag="t")
+            for g in range(passes_of(i)):
+                for u in range(2):
+                    nc.tensor.transpose(
+                        bank[:, g, u, :], words[:, 2 * g * P + u : 2 * (g + 1) * P : 2], ident_f32[:]
+                    )
+            e_banks[n] = bank
+
+        def regroup(n):
+            passes = passes_of(n // HEADS)
+            grouped = work.tile([P, passes * K_PASS], BF16, name="grouped", align_bytes=64)
+            nc.scalar.copy(
+                out=grouped[:].bitcast(F32).rearrange("p (g r u) -> p g r u", g=passes, u=2),
+                in_=e_banks[n][:].rearrange("p g u r -> p g r u"),
+            )
+            e_grouped[n] = grouped
+
+        def quantise(n):
+            passes = passes_of(n // HEADS)
+            codes = work.tile([P, passes * P], U32, name="codes", align_bytes=64)
+            scales = work.tile([P, passes * P], U8, name="scales", align_bytes=64)
+            nc.vector.quantize_mx(out=codes[:].bitcast(FP8X4), scales=scales[:], in_=e_grouped[n][:])
+            e_codes[n] = codes
+            e_scales[n] = scales
+
+        def attend(n):
+            i, h = divmod(n, HEADS)
+            m, half = divmod(n, 2)
+            if half == 0:
+                o_banks[m] = ps_o.tile([P, 2, PAIR_DIM], F32, name="o_bank")
+            features = slice((h // 2) * PAIR_DIM, (h // 2 + 1) * PAIR_DIM)
+            for g in range(passes_of(i)):
+                queries = slice(g * P, (g + 1) * P)
+                nc.tensor.matmul_mx(
+                    out=o_banks[m][:, half, :],
+                    lhsT=e_codes[n][:, queries].bitcast(FP8X4),
+                    lhsT_scale=e_scales[n][:, queries],
+                    rhs=v_codes[g][:, features].bitcast(FP8X4),
+                    rhs_scale=v_scales[g][:, features],
+                    start=(g == 0),
+                    stop=(g == passes_of(i) - 1),
+                )
+
+        factors = {}
+        seconds = {}
+        xs = {}
+        rstds = {}
+
+        def weigh(m):
+            sums = row_sums[m]
+            total = sums[:, :, 0]
+            if passes_of(m // 2) == 2:
+                added = small.tile([P, 2], F32, name="added")
+                nc.gpsimd.tensor_tensor(out=added[:], in0=sums[:, :, 0], in1=sums[:, :, 1], op=ALU.add)
+                total = added[:]
+            inverse = small.tile([P, 2], F32, name="inverse")
+            nc.gpsimd.tensor_tensor(out=inverse[:], in0=total, in1=minus_one[:], op=ALU.pow)
+            factor = small.tile([P, 2], F32, name="factor")
+            nc.gpsimd.tensor_tensor(out=factor[:], in0=inverse[:], in1=signs[:], op=ALU.mult)
+            factors[m] = factor
+
+        def scale_second(m):
+            second = work.tile([P, PAIR_DIM], F32, name="second")
+            nc.scalar.activation(
+                out=second[:], in_=o_banks[m][:, 1, :], func=FUNC.Copy, scale=factors[m][:, 1:2]
+            )
+            seconds[m] = second
+
+        def combine(m):
+            x = work.tile([P, PAIR_DIM], F32, name="x")
+            nc.vector.scalar_tensor_tensor(
+                out=x[:],
+                in0=o_banks[m][:, 0, :],
+                scalar=factors[m][:, 0:1],
+                in1=seconds[m][:],
+                op0=ALU.mult,
+                op1=ALU.add,
+            )
+            xs[m] = x
+
+        def measure(m):
+            squares = work.tile([P, PAIR_DIM], F32, name="squares")
+            sum_sq = small.tile([P, 1], F32, name="sum_sq")
+            nc.scalar.activation(out=squares[:], in_=xs[m][:], func=FUNC.Square, accum_out=sum_sq[:])
+            floored = small.tile([P, 1], F32, name="floored")
+            nc.gpsimd.tensor_scalar_add(out=floored[:], in0=sum_sq[:], scalar1=PAIR_DIM * EPS)
+            rstd = small.tile([P, 1], F32, name="rstd")
+            nc.gpsimd.tensor_tensor(out=rstd[:], in0=floored[:], in1=minus_half[:], op=ALU.pow)
+            rstds[m] = rstd
+
+        def finish(m):
+            i, pair = divmod(m, 2)
+            y = work.tile([P, PAIR_DIM], F32, name="y")
+            nc.vector.scalar_tensor_tensor(
+                out=y[:],
+                in0=xs[m][:],
+                scalar=rstds[m][:, 0:1],
+                in1=gain[:],
+                op0=ALU.mult,
+                op1=ALU.mult,
+            )
+            nc.sync.dma_start(
+                out=out_rows[:, i, pair * PAIR_DIM : (pair + 1) * PAIR_DIM], in_=y[:]
+            )
+
+        def run(stage, index, count):
+            if 0 <= index < count:
+                stage(index)
+
+        def run_pair(stage, n, lag):
+            if (n - lag) % 2 == 0:
+                run(stage, (n - lag) // 2, PAIR_UNITS)
+
+        def tick(n):
+            run_pair(scale_second, n, 5)
+            run_pair(measure, n, 7)
+            run(exponent, n, UNITS)
+            run(regroup, n - 1, UNITS)
+            if n == LAM_TICK + 1:
+                lam_products()
+            if n == LAM_TICK + 2:
+                scale_gain()
+            if n == LAM_TICK + 3:
+                lam_dots()
+            if n == LAM_TICK + 4:
+                lam_signs()
+            run(row_tops, n + 1, UNITS)
+            run(quantise, n - 2, UNITS)
+            run(shift, n + 1, UNITS)
+            run_pair(combine, n, 5)
+            run_pair(finish, n, 11)
+            if n % HEADS == 1:
+                run(copy_rows, n // HEADS + 2, Q_TILES)
+            round_of_pass = HEADS * TILES_PER_PASS
+            if (n + 1) % round_of_pass == 0:
+                run(regroup_values, (n + 1) // round_of_pass, PASSES)
+            if n % round_of_pass == 0:
+                run(quantise_values, n // round_of_pass, PASSES)
+            run_pair(weigh, n, 2)
+            run(scores, n + 2, UNITS)
+            run(turn, n, UNITS)
+            run(attend, n - 2, UNITS)
+            if n % HEADS == 0:
+                run(turn_rows, n // HEADS + 2, Q_TILES)
+            if n == LAM_TICK:
+                spread_vectors()
+
+        first_tick = -2 * HEADS
+        last_tick = 2 * (PAIR_UNITS - 1) + 11
+        with tc.manual_schedule():
+            for n in range(first_tick, last_tick + 1):
+                tick(n)

@@ -6,6 +6,7 @@ from concourse.masks import make_identity
 
 BF16 = mybir.dt.bfloat16
 F32 = mybir.dt.float32
+I32 = mybir.dt.int32
 U32 = mybir.dt.uint32
 U8 = mybir.dt.uint8
 FP8X4 = mybir.dt.float8_e4m3fn_x4
@@ -16,29 +17,52 @@ AXIS = mybir.AxisListType
 P = 128
 SEQ = 1024
 HEADS = 4
+PAIRS = HEADS // 2
 DIM = 128
 ROW = HEADS * DIM
 PAIR_DIM = 2 * DIM
 PACK = 4
 K_PASS = P * PACK
 TILES_PER_PASS = K_PASS // P
+TILE_PARTS = P // TILES_PER_PASS
 PASSES = SEQ // K_PASS
 Q_TILES = SEQ // P
-UNITS = Q_TILES * HEADS
-PAIR_UNITS = UNITS // 2
 
 SCALE = 1.0 / math.sqrt(DIM)
 LAMBDA_INIT = 0.8 - 0.6 * math.exp(-0.3 * 12)
 NEG_INF = -1e30
 EPS = 1e-5
+X_TILES = 6
 
-LAM_TICK = -3
+TILE_ORDER = (0, 2, 4, 1, 5, 6, 7, 3)
+TOGETHER = {0: 4, 1: 2, 2: 2}
+STEPS = [
+    (i, tuple(range(h, h + TOGETHER.get(i, 1))))
+    for i in TILE_ORDER
+    for h in range(0, HEADS, TOGETHER.get(i, 1))
+]
 
 FLOPS = 2 * HEADS * (512 * 512 + 512 * 1024) * (DIM + PAIR_DIM)
 
 
-def passes_of(q_tile):
-    return q_tile // TILES_PER_PASS + 1
+def partner(i):
+    return 6 - i
+
+
+def shares(i):
+    return i in (4, 5, 6)
+
+
+def passes_of(i):
+    return 0 if i < 3 else 1 if i == 3 else 2
+
+
+def segments(i):
+    if i < TILES_PER_PASS:
+        owner, number = (3, 0) if i == 3 else (partner(i), 1)
+        return [(0, 0, (i + 1) * P, i * P, owner, number)]
+    width = (i - TILES_PER_PASS + 1) * P
+    return [(0, 0, K_PASS, None, i, 0), (1, K_PASS - width, width, 0, i, 1)]
 
 
 def tile_refphi4flashdiffattention_pa_kernel(
@@ -49,16 +73,19 @@ def tile_refphi4flashdiffattention_pa_kernel(
     q_rows = q.rearrange("b (j p) h d -> p (b j) (h d)", p=P)
     k_rows = k.rearrange("b (j p) h d -> p (b j) (h d)", p=P)
     out_rows = out.rearrange("b (j p) h d -> p (b j) (h d)", p=P)
-    v_rows = v.rearrange("b (g p t) h d -> p (b g) (t h d)", p=P, t=PACK)
+    v_pass_rows = v.rearrange("b (g p t) h d -> p (b g) (t h d)", p=P, t=PACK)
+    v_tile_rows = v.rearrange("b (j p t) h d -> p (b j) (t h d)", p=TILE_PARTS, t=PACK)
 
     with ExitStack() as stack:
         keep = stack.enter_context(tc.tile_pool(name="keep", bufs=1))
-        work = stack.enter_context(tc.tile_pool(name="work", bufs=4))
+        work = stack.enter_context(tc.tile_pool(name="work", bufs=6))
         small = stack.enter_context(tc.tile_pool(name="small", bufs=6))
         ps_s = stack.enter_context(tc.psum_pool(name="ps_s", bufs=4))
         ps_t = stack.enter_context(tc.psum_pool(name="ps_t", bufs=2))
         ps_o = stack.enter_context(tc.psum_pool(name="ps_o", bufs=2))
 
+        table = keep.tile([P, 1], F32, name="table")
+        nc.vector.memset(table[:], 0.0)
         first_row = keep.tile([P, 4 * DIM + PAIR_DIM], BF16, name="first_row")
         nc.vector.memset(first_row[:], 0.0)
         for slot, vector in enumerate((lambda_q1, lambda_q2, lambda_k1, lambda_k2)):
@@ -66,6 +93,8 @@ def tile_refphi4flashdiffattention_pa_kernel(
                 out=first_row[0:1, slot * DIM : (slot + 1) * DIM], in_=vector.unsqueeze(0)
             )
         nc.scalar.dma_start(out=first_row[0:1, 4 * DIM :], in_=subln_weight.unsqueeze(0))
+
+        nc.scalar.activation(out=table[:], in_=table[:], func=FUNC.Exp)
 
         q_sb = [keep.tile([P, ROW], BF16, name="q_sb%d" % j) for j in range(Q_TILES)]
         k_sb = [keep.tile([P, ROW], BF16, name="k_sb%d" % j) for j in range(Q_TILES)]
@@ -75,13 +104,18 @@ def tile_refphi4flashdiffattention_pa_kernel(
             nc.sync.dma_start(out=k_sb[j][:], in_=k_rows[:, j, :])
             nc.sync.dma_start(out=q_sb[j][:], in_=q_rows[:, j, :])
 
-        def load_values(g):
-            nc.sync.dma_start(out=v_raw[g][:].rearrange("p t c -> p (t c)"), in_=v_rows[:, g, :])
-
-        for j in range(Q_TILES):
+        for j in range(5):
             load_rows(j)
-            if j % TILES_PER_PASS == 1:
-                load_values(j // TILES_PER_PASS)
+        nc.sync.dma_start(out=v_raw[0][:].rearrange("p t c -> p (t c)"), in_=v_pass_rows[:, 0, :])
+        for b in range(TILES_PER_PASS):
+            nc.sync.dma_start(
+                out=v_raw[1][b * TILE_PARTS : (b + 1) * TILE_PARTS, :, :].rearrange(
+                    "p t c -> p (t c)"
+                ),
+                in_=v_tile_rows[:, Q_TILES - 1 - b, :],
+            )
+        for j in range(5, Q_TILES):
+            load_rows(j)
 
         ident_bf = keep.tile([P, P], BF16, name="ident_bf")
         make_identity(nc, ident_bf[:])
@@ -105,14 +139,18 @@ def tile_refphi4flashdiffattention_pa_kernel(
         minus_half = keep.tile([P, 1], F32, name="minus_half")
         nc.gpsimd.memset(minus_half[:], -0.5)
 
-        e_tiles = []
-        for i in range(Q_TILES):
-            width = passes_of(i) * K_PASS
-            e_tile = keep.tile([P, HEADS, width], BF16, name="e_tile%d" % i)
-            seen = (i + 1) * P
-            if seen < width:
-                nc.vector.memset(e_tile[:, :, seen:width], 0.0)
-            e_tiles.append(e_tile)
+        x_tiles = []
+        for index in range(X_TILES):
+            x_tile = keep.tile([P, PAIR_DIM + 1], F32, name="x_tile%d" % index)
+            nc.gpsimd.tensor_scalar(
+                out=x_tile[:, PAIR_DIM : PAIR_DIM + 1],
+                in0=minus_half[:],
+                scalar1=0.0,
+                scalar2=math.sqrt(PAIR_DIM * EPS),
+                op0=ALU.mult,
+                op1=ALU.add,
+            )
+            x_tiles.append(x_tile)
 
         ones = keep.tile([P, P], BF16, name="ones")
         nc.vector.memset(ones[:], 1.0)
@@ -128,7 +166,7 @@ def tile_refphi4flashdiffattention_pa_kernel(
         spread_banks = {}
 
         def spread_vectors():
-            lam_bank = ps_s.tile([P, 4, DIM], F32, name="lam_bank", tag="s_bank")
+            lam_bank = ps_o.tile([P, 4, DIM], F32, name="lam_bank", tag="o_bank")
             nc.tensor.matmul(
                 out=lam_bank[:].rearrange("p s d -> p (s d)"),
                 lhsT=ones[:],
@@ -136,7 +174,7 @@ def tile_refphi4flashdiffattention_pa_kernel(
                 start=True,
                 stop=True,
             )
-            weight_bank = ps_s.tile([P, PAIR_DIM], F32, name="weight_bank", tag="s_bank")
+            weight_bank = ps_o.tile([P, PAIR_DIM], F32, name="weight_bank", tag="o_bank")
             nc.tensor.matmul(
                 out=weight_bank[:], lhsT=ones[:], rhs=first_row[:, 4 * DIM :], start=True, stop=True
             )
@@ -182,11 +220,19 @@ def tile_refphi4flashdiffattention_pa_kernel(
         v_scales = [
             keep.tile([P, ROW], U8, name="v_scales%d" % g, align_bytes=64) for g in range(PASSES)
         ]
+        v_part = {}
+        for i in (2, 4, 1, 5, 0, 6):
+            v_part[i] = keep.tile([P, ROW], U32, name="v_part%d" % i, align_bytes=64)
+            nc.gpsimd.memset(v_part[i][:], 0)
 
         def regroup_values(g):
-            nc.vector.tensor_copy(
+            nc.gpsimd.tensor_scalar(
                 out=v_grouped[g][:].rearrange("p (c i t) -> p c t i", i=4, t=PACK),
-                in_=v_raw[g][:].rearrange("p t (c i) -> p c t i", i=4),
+                in0=v_raw[g][:].rearrange("p t (c i) -> p c t i", i=4),
+                scalar1=1.0,
+                scalar2=0.0,
+                op0=ALU.mult,
+                op1=ALU.add,
             )
 
         def quantise_values(g):
@@ -194,25 +240,43 @@ def tile_refphi4flashdiffattention_pa_kernel(
                 out=v_codes[g][:].bitcast(FP8X4), scales=v_scales[g][:], in_=v_grouped[g][:]
             )
 
+        def part_values(i):
+            g = i // TILES_PER_PASS
+            first = 0 if g == 0 else (Q_TILES - 1 - i) * TILE_PARTS
+            last = (i + 1) * TILE_PARTS if g == 0 else P
+            nc.sync.dma_start(
+                out=v_part[i][first:last, :].bitcast(I32), in_=v_codes[g][first:last, :].bitcast(I32)
+            )
+
         q_turned = [keep.tile([P, HEADS, P], BF16, name="q_turned%d" % j) for j in range(Q_TILES)]
         k_turned = [keep.tile([P, HEADS, K_PASS], BF16, name="k_turned%d" % g) for g in range(PASSES)]
         rows_ps = {}
 
         def turn_rows(j):
-            bank = ps_t.tile([P, 2, HEADS, P], BF16, name="rows_bank", tag="t")
-            for h in range(HEADS):
-                cols = slice(h * DIM, (h + 1) * DIM)
-                nc.tensor.transpose(bank[:, 0, h, :], q_sb[j][:, cols], ident_bf[:])
-                nc.tensor.transpose(bank[:, 1, h, :], k_sb[j][:, cols], ident_bf[:])
-            rows_ps[j] = bank
+            pool, tag = (ps_o, "o_bank") if j in (1, 3) else (ps_t, "t")
+            k_bank = pool.tile([P, HEADS, P], BF16, name="k_bank", tag=tag)
+            q_bank = pool.tile([P, HEADS, P], BF16, name="q_bank", tag=tag)
+            for bank, rows in ((k_bank, k_sb[j]), (q_bank, q_sb[j])):
+                for h in range(HEADS):
+                    nc.tensor.transpose(
+                        bank[:, h, :], rows[:, h * DIM : (h + 1) * DIM], ident_bf[:]
+                    )
+            rows_ps[j] = (k_bank, q_bank)
 
         def copy_rows(j):
-            g, t = divmod(j, TILES_PER_PASS)
-            nc.vector.tensor_copy(out=q_turned[j][:], in_=rows_ps[j][:, 0, :, :])
-            nc.vector.tensor_copy(
-                out=k_turned[g][:, :, t * P : (t + 1) * P], in_=rows_ps[j][:, 1, :, :]
-            )
+            g = j // TILES_PER_PASS
+            t = j if g == 0 else Q_TILES - 1 - j
+            copy_q = nc.scalar.copy if j < 5 else nc.vector.tensor_copy
+            k_bank, q_bank = rows_ps[j]
+            nc.vector.tensor_copy(out=k_turned[g][:, :, t * P : (t + 1) * P], in_=k_bank[:])
+            copy_q(out=q_turned[j][:], in_=q_bank[:])
 
+        e_tiles = {}
+        for i in (4, 5, 6, 7, 3):
+            for h in range(HEADS):
+                e_tiles[i, h] = keep.tile(
+                    [P, passes_of(i), 2, K_PASS // 2], BF16, name="e_tile%d_%d" % (i, h)
+                )
         s_banks = {}
         tops = {}
         shifts = {}
@@ -224,43 +288,58 @@ def tile_refphi4flashdiffattention_pa_kernel(
         o_banks = {}
 
         def scores(n):
-            i, h = divmod(n, HEADS)
-            banks = []
-            for g in range(passes_of(i)):
-                width = min(i + 1 - g * TILES_PER_PASS, TILES_PER_PASS) * P
-                holds_diagonal = g == passes_of(i) - 1
-                bank = ps_s.tile([P, K_PASS], F32, name="s_bank")
-                nc.tensor.matmul(
-                    out=bank[:, 0:width],
-                    lhsT=q_turned[i][:, h, :],
-                    rhs=k_turned[g][:, h, 0:width],
-                    start=True,
-                    stop=not holds_diagonal,
-                )
-                if holds_diagonal:
+            i, heads = STEPS[n]
+            pieces = []
+            bank = None
+            column = K_PASS
+            for h in heads:
+                for s, (g, first, width, diagonal, owner, number) in enumerate(segments(i)):
+                    if column + width > K_PASS:
+                        bank = ps_s.tile([P, K_PASS], F32, name="s_bank")
+                        column = 0
                     nc.tensor.matmul(
-                        out=bank[:, width - P : width],
-                        lhsT=ident_bf[:],
-                        rhs=mask_bf[:],
-                        start=False,
-                        stop=True,
+                        out=bank[:, column : column + width],
+                        lhsT=q_turned[i][:, h, :],
+                        rhs=k_turned[g][:, h, first : first + width],
+                        start=True,
+                        stop=diagonal is None,
                     )
-                banks.append((bank, width))
-            s_banks[n] = banks
+                    if diagonal is not None:
+                        nc.tensor.matmul(
+                            out=bank[:, column + diagonal : column + diagonal + P],
+                            lhsT=ident_bf[:],
+                            rhs=mask_bf[:],
+                            start=False,
+                            stop=True,
+                        )
+                    pieces.append((bank, column, h, s))
+                    column += width
+            s_banks[n] = pieces
 
         def row_tops(n):
-            top = small.tile([P, PASSES], F32, name="top")
-            for g, (bank, width) in enumerate(s_banks[n]):
+            i, heads = STEPS[n]
+            top = small.tile([P, HEADS], F32, name="top")
+            pieces = s_banks[n]
+            index = 0
+            while index < len(pieces):
+                bank, column, h, s = pieces[index]
+                width = segments(i)[s][2]
+                count = sum(1 for piece in pieces if piece[0] is bank)
                 nc.vector.tensor_reduce(
-                    out=top[:, g : g + 1], in_=bank[:, 0:width], axis=AXIS.X, op=ALU.max
+                    out=top[:, index : index + count],
+                    in_=bank[:, 0 : count * width].rearrange("p (c w) -> p c w", c=count),
+                    axis=AXIS.X,
+                    op=ALU.max,
                 )
+                index += count
             tops[n] = top
 
         def shift(n):
-            bias = small.tile([P, 1], F32, name="bias")
-            if len(s_banks[n]) == 2:
+            i, heads = STEPS[n]
+            bias = small.tile([P, HEADS], F32, name="bias")
+            if len(segments(i)) == 2:
                 nc.vector.tensor_scalar(
-                    out=bias[:],
+                    out=bias[:, 0:1],
                     in0=tops[n][:, 0:1],
                     scalar1=tops[n][:, 1:2],
                     scalar2=-SCALE,
@@ -268,37 +347,49 @@ def tile_refphi4flashdiffattention_pa_kernel(
                     op1=ALU.mult,
                 )
             else:
-                nc.vector.tensor_scalar_mul(out=bias[:], in0=tops[n][:, 0:1], scalar1=-SCALE)
+                nc.vector.tensor_scalar_mul(
+                    out=bias[:, 0 : len(heads)], in0=tops[n][:, 0 : len(heads)], scalar1=-SCALE
+                )
             shifts[n] = bias
 
         def exponent(n):
-            i, h = divmod(n, HEADS)
-            m, half = divmod(n, 2)
-            if half == 0:
-                row_sums[m] = small.tile([P, 2, passes_of(i)], F32, name="row_sum")
-            for g, (bank, width) in enumerate(s_banks[n]):
+            i, heads = STEPS[n]
+            parts = segments(i)
+            for bank, column, h, s in s_banks[n]:
+                pair, half = divmod(h, 2)
+                if (i, pair) not in row_sums:
+                    row_sums[i, pair] = keep.tile(
+                        [P, 2, len(parts)], F32, name="row_sum%d_%d" % (i, pair)
+                    )
+                g, first, width, diagonal, owner, number = parts[s]
+                index = h - heads[0]
                 nc.scalar.activation(
-                    out=e_tiles[i][:, h, g * K_PASS : g * K_PASS + width],
-                    in_=bank[:, 0:width],
+                    out=e_tiles[owner, h][
+                        :, number, :, first // 2 : (first + width) // 2
+                    ].rearrange("q u (p e) -> q u p e", e=2),
+                    in_=bank[:, column : column + width].rearrange(
+                        "q (p u e) -> q u p e", u=2, e=2
+                    ),
                     func=FUNC.Exp,
-                    bias=shifts[n][:, 0:1],
+                    bias=shifts[n][:, index : index + 1],
                     scale=SCALE,
-                    accum_out=row_sums[m][:, half, g : g + 1],
+                    accum_out=row_sums[i, pair][:, half, s : s + 1],
                 )
 
         def turn(n):
-            i, h = divmod(n, HEADS)
-            words = e_tiles[i][:, h, :].bitcast(F32)
+            i, (h,) = STEPS[n]
             bank = ps_t.tile([P, passes_of(i), 2, P], F32, name="e_bank", tag="t")
-            for g in range(passes_of(i)):
+            for number in range(passes_of(i)):
                 for u in range(2):
                     nc.tensor.transpose(
-                        bank[:, g, u, :], words[:, 2 * g * P + u : 2 * (g + 1) * P : 2], ident_f32[:]
+                        bank[:, number, u, :],
+                        e_tiles[i, h][:, number, u, :].bitcast(F32),
+                        ident_f32[:],
                     )
             e_banks[n] = bank
 
         def regroup(n):
-            passes = passes_of(n // HEADS)
+            passes = passes_of(STEPS[n][0])
             grouped = work.tile([P, passes * K_PASS], BF16, name="grouped", align_bytes=64)
             nc.scalar.copy(
                 out=grouped[:].bitcast(F32).rearrange("p (g r u) -> p g r u", g=passes, u=2),
@@ -307,85 +398,109 @@ def tile_refphi4flashdiffattention_pa_kernel(
             e_grouped[n] = grouped
 
         def quantise(n):
-            passes = passes_of(n // HEADS)
+            passes = passes_of(STEPS[n][0])
             codes = work.tile([P, passes * P], U32, name="codes", align_bytes=64)
             scales = work.tile([P, passes * P], U8, name="scales", align_bytes=64)
             nc.vector.quantize_mx(out=codes[:].bitcast(FP8X4), scales=scales[:], in_=e_grouped[n][:])
             e_codes[n] = codes
             e_scales[n] = scales
 
-        def attend(n):
-            i, h = divmod(n, HEADS)
-            m, half = divmod(n, 2)
+        def attend(i, pair, half, n, passes):
             if half == 0:
-                o_banks[m] = ps_o.tile([P, 2, PAIR_DIM], F32, name="o_bank")
-            features = slice((h // 2) * PAIR_DIM, (h // 2 + 1) * PAIR_DIM)
-            for g in range(passes_of(i)):
-                queries = slice(g * P, (g + 1) * P)
+                o_banks[i, pair] = ps_o.tile([P, 2, PAIR_DIM], F32, name="o_bank")
+            features = slice(pair * PAIR_DIM, (pair + 1) * PAIR_DIM)
+            for index, (number, codes, scales) in enumerate(passes):
+                queries = slice(number * P, (number + 1) * P)
                 nc.tensor.matmul_mx(
-                    out=o_banks[m][:, half, :],
+                    out=o_banks[i, pair][:, half, :],
                     lhsT=e_codes[n][:, queries].bitcast(FP8X4),
                     lhsT_scale=e_scales[n][:, queries],
-                    rhs=v_codes[g][:, features].bitcast(FP8X4),
-                    rhs_scale=v_scales[g][:, features],
-                    start=(g == 0),
-                    stop=(g == passes_of(i) - 1),
+                    rhs=codes[:, features].bitcast(FP8X4),
+                    rhs_scale=scales[:, features],
+                    start=(index == 0),
+                    stop=(index == len(passes) - 1),
                 )
 
+        def attend_pair(c):
+            i, (h,) = STEPS[c]
+            pair = h // 2
+            passes = [(0, v_codes[0], v_scales[0])]
+            if i == 7:
+                passes.append((1, v_codes[1], v_scales[1]))
+            if shares(i):
+                passes.append((1, v_part[i], v_scales[1]))
+            for half in range(2):
+                attend(i, pair, half, c - 1 + half, passes)
+                if shares(i):
+                    low = partner(i)
+                    attend(low, pair, half, c - 1 + half, [(1, v_part[low], v_scales[0])])
+
         factors = {}
-        seconds = {}
+        firsts = {}
         xs = {}
         rstds = {}
 
-        def weigh(m):
-            sums = row_sums[m]
+        def weigh(i, pair):
+            sums = row_sums[i, pair]
             total = sums[:, :, 0]
-            if passes_of(m // 2) == 2:
+            if len(segments(i)) == 2:
                 added = small.tile([P, 2], F32, name="added")
                 nc.gpsimd.tensor_tensor(out=added[:], in0=sums[:, :, 0], in1=sums[:, :, 1], op=ALU.add)
                 total = added[:]
             inverse = small.tile([P, 2], F32, name="inverse")
-            nc.gpsimd.tensor_tensor(out=inverse[:], in0=total, in1=minus_one[:], op=ALU.pow)
-            factor = small.tile([P, 2], F32, name="factor")
+            if i in (3,):
+                nc.vector.reciprocal(out=inverse[:], in_=total)
+            else:
+                nc.gpsimd.tensor_tensor(out=inverse[:], in0=total, in1=minus_one[:], op=ALU.pow)
+            factor = keep.tile([P, 2], F32, name="factor%d_%d" % (i, pair))
             nc.gpsimd.tensor_tensor(out=factor[:], in0=inverse[:], in1=signs[:], op=ALU.mult)
-            factors[m] = factor
+            factors[i, pair] = factor
 
-        def scale_second(m):
-            second = work.tile([P, PAIR_DIM], F32, name="second")
+        def scale_first(i, pair):
+            scaled = work.tile([P, PAIR_DIM], F32, name="scaled")
             nc.scalar.activation(
-                out=second[:], in_=o_banks[m][:, 1, :], func=FUNC.Copy, scale=factors[m][:, 1:2]
+                out=scaled[:],
+                in_=o_banks[i, pair][:, 0, :],
+                func=FUNC.Copy,
+                scale=factors[i, pair][:, 0:1],
             )
-            seconds[m] = second
+            firsts[i, pair] = scaled
 
-        def combine(m):
-            x = work.tile([P, PAIR_DIM], F32, name="x")
+        def combine(i, pair):
+            x = x_tiles[len(xs) % X_TILES]
             nc.vector.scalar_tensor_tensor(
-                out=x[:],
-                in0=o_banks[m][:, 0, :],
-                scalar=factors[m][:, 0:1],
-                in1=seconds[m][:],
+                out=x[:, 0:PAIR_DIM],
+                in0=o_banks[i, pair][:, 1, :],
+                scalar=factors[i, pair][:, 1:2],
+                in1=firsts[i, pair][:],
                 op0=ALU.mult,
                 op1=ALU.add,
             )
-            xs[m] = x
+            xs[i, pair] = x
 
-        def measure(m):
-            squares = work.tile([P, PAIR_DIM], F32, name="squares")
+        def measure(i, pair):
+            squares = work.tile([P, PAIR_DIM + 1], F32, name="squares")
             sum_sq = small.tile([P, 1], F32, name="sum_sq")
-            nc.scalar.activation(out=squares[:], in_=xs[m][:], func=FUNC.Square, accum_out=sum_sq[:])
-            floored = small.tile([P, 1], F32, name="floored")
-            nc.gpsimd.tensor_scalar_add(out=floored[:], in0=sum_sq[:], scalar1=PAIR_DIM * EPS)
+            x = xs[i, pair][:]
+            if i in (0, 1, 2):
+                nc.vector.scalar_tensor_tensor(
+                    out=squares[:], in0=x, scalar=1.0, in1=x, op0=ALU.mult, op1=ALU.mult,
+                    accum_out=sum_sq[:],
+                )
+            else:
+                nc.scalar.activation(
+                    out=squares[:], in_=x, func=FUNC.Square, accum_out=sum_sq[:]
+                )
             rstd = small.tile([P, 1], F32, name="rstd")
-            nc.gpsimd.tensor_tensor(out=rstd[:], in0=floored[:], in1=minus_half[:], op=ALU.pow)
-            rstds[m] = rstd
+            nc.gpsimd.tensor_tensor(out=rstd[:], in0=sum_sq[:], in1=minus_half[:], op=ALU.pow)
+            rstds[i, pair] = rstd
 
-        def finish(m):
-            i, pair = divmod(m, 2)
+        def finish(i, pair):
             y = work.tile([P, PAIR_DIM], F32, name="y")
             nc.vector.scalar_tensor_tensor(
                 out=y[:],
-                in0=xs[m][:],
-                scalar=rstds[m][:, 0:1],
+                in0=xs[i, pair][:, 0:PAIR_DIM],
+                scalar=rstds[i, pair][:, 0:1],
                 in1=gain[:],
                 op0=ALU.mult,
                 op1=ALU.mult,
@@ -394,50 +509,52 @@ def tile_refphi4flashdiffattention_pa_kernel(
                 out=out_rows[:, i, pair * PAIR_DIM : (pair + 1) * PAIR_DIM], in_=y[:]
             )
 
-        def run(stage, index, count):
-            if 0 <= index < count:
-                stage(index)
+        def closes(n):
+            return 0 <= n < len(STEPS) and passes_of(STEPS[n][0]) > 0
 
-        def run_pair(stage, n, lag):
-            if (n - lag) % 2 == 0:
-                run(stage, (n - lag) // 2, PAIR_UNITS)
+        def run(stage, n, closing=False):
+            if 0 <= n < len(STEPS) and (not closing or closes(n)):
+                stage(n)
+
+        def run_pair(stage, c):
+            if closes(c) and STEPS[c][1][0] % 2 == 1:
+                i, (h,) = STEPS[c]
+                stage(i, h // 2)
+                if shares(i):
+                    stage(partner(i), h // 2)
+
+        ROWS = {-4:(0,),-3:(1,),-2:(2,),-1:(3,),0:(4,),4:(5,),7:(6,),11:(7,)}
 
         def tick(n):
-            run_pair(scale_second, n, 5)
-            run_pair(measure, n, 7)
-            run(exponent, n, UNITS)
-            run(regroup, n - 1, UNITS)
-            if n == LAM_TICK + 1:
-                lam_products()
-            if n == LAM_TICK + 2:
-                scale_gain()
-            if n == LAM_TICK + 3:
-                lam_dots()
-            if n == LAM_TICK + 4:
-                lam_signs()
-            run(row_tops, n + 1, UNITS)
-            run(quantise, n - 2, UNITS)
-            run(shift, n + 1, UNITS)
-            run_pair(combine, n, 5)
-            run_pair(finish, n, 11)
-            if n % HEADS == 1:
-                run(copy_rows, n // HEADS + 2, Q_TILES)
-            round_of_pass = HEADS * TILES_PER_PASS
-            if (n + 1) % round_of_pass == 0:
-                run(regroup_values, (n + 1) // round_of_pass, PASSES)
-            if n % round_of_pass == 0:
-                run(quantise_values, n // round_of_pass, PASSES)
-            run_pair(weigh, n, 2)
-            run(scores, n + 2, UNITS)
-            run(turn, n, UNITS)
-            run(attend, n - 2, UNITS)
-            if n % HEADS == 0:
-                run(turn_rows, n // HEADS + 2, Q_TILES)
-            if n == LAM_TICK:
-                spread_vectors()
+            run(exponent, n)
+            run(regroup, n - 1, closing=True)
+            run_pair(scale_first, n - 3)
+            run_pair(lambda i, p: measure(i, p) if i not in (0, 1, 2) else None, n - 5)
+            run(row_tops, n + 1)
+            run(quantise, n - 2, closing=True)
+            run_pair(combine, n - 4)
+            run(shift, n + 1)
+            run_pair(lambda i, p: measure(i, p) if i in (0, 1, 2) else None, n - 5)
+            run_pair(finish, n - 7)
+            run_pair(weigh, n - 1)
+            for j in ROWS.get(n - 1, ()):
+                copy_rows(j)
+            run(scores, n + 2)
+            run(turn, n, closing=True)
+            if closes(n - 2) and STEPS[n - 2][1][0] % 2 == 1:
+                attend_pair(n - 2)
+            for j in ROWS.get(n, ()):
+                turn_rows(j)
+            for once in ONCE.get(n, []):
+                once()
 
-        first_tick = -2 * HEADS
-        last_tick = 2 * (PAIR_UNITS - 1) + 11
+        ONCE = {}
+        fns = dict(spread=spread_vectors, prod=lam_products, gain=scale_gain, dots=lam_dots, signs=lam_signs,
+            rv0=lambda: regroup_values(0), rv1=lambda: regroup_values(1), qv0=lambda: quantise_values(0), qv1=lambda: quantise_values(1),
+            p0=lambda: part_values(0), p1=lambda: part_values(1), p2=lambda: part_values(2), p4=lambda: part_values(4), p5=lambda: part_values(5), p6=lambda: part_values(6))
+        for nm, tk in [('spread',0),('prod',1),('gain',1),('rv0',0),('rv1',2),('dots',3),('signs',4),('qv0',3),('p2',3),('p1',3),('p0',3),('qv1',4),('p4',4),('p5',4),('p6',4)]:
+            ONCE.setdefault(tk, []).append(fns[nm])
+
         with tc.manual_schedule():
-            for n in range(first_tick, last_tick + 1):
+            for n in range(-6, len(STEPS) + 7 + 1):
                 tick(n)

@@ -226,14 +226,17 @@ def tile_refphi4flashdiffattention_pa_kernel(
             nc.gpsimd.memset(v_part[i][:], 0)
 
         def regroup_values(g):
-            nc.gpsimd.tensor_scalar(
-                out=v_grouped[g][:].rearrange("p (c i t) -> p c t i", i=4, t=PACK),
-                in0=v_raw[g][:].rearrange("p t (c i) -> p c t i", i=4),
-                scalar1=1.0,
-                scalar2=0.0,
-                op0=ALU.mult,
-                op1=ALU.add,
-            )
+            w = 160
+            if w < ROW:
+              nc.vector.tensor_copy(
+                out=v_grouped[g][:,0:(ROW-w)*4].rearrange("p (c i t) -> p c t i", i=4, t=PACK),
+                in_=v_raw[g][:,:,0:ROW-w].rearrange("p t (c i) -> p c t i", i=4),
+              )
+            if w:
+              nc.scalar.copy(
+                out=v_grouped[g][:,(ROW-w)*4:].rearrange("p (c i t) -> p c t i", i=4, t=PACK),
+                in_=v_raw[g][:,:,ROW-w:].rearrange("p t (c i) -> p c t i", i=4),
+              )
 
         def quantise_values(g):
             nc.vector.quantize_mx(
@@ -436,6 +439,7 @@ def tile_refphi4flashdiffattention_pa_kernel(
                     attend(low, pair, half, c - 1 + half, [(1, v_part[low], v_scales[0])])
 
         factors = {}
+        inverses = {}
         firsts = {}
         xs = {}
         rstds = {}
@@ -447,13 +451,15 @@ def tile_refphi4flashdiffattention_pa_kernel(
                 added = small.tile([P, 2], F32, name="added")
                 nc.gpsimd.tensor_tensor(out=added[:], in0=sums[:, :, 0], in1=sums[:, :, 1], op=ALU.add)
                 total = added[:]
-            inverse = small.tile([P, 2], F32, name="inverse")
+            inverse = keep.tile([P, 2], F32, name="inverse%d_%d" % (i, pair))
             if i in (3,):
                 nc.vector.reciprocal(out=inverse[:], in_=total)
             else:
                 nc.gpsimd.tensor_tensor(out=inverse[:], in0=total, in1=minus_one[:], op=ALU.pow)
-            factor = keep.tile([P, 2], F32, name="factor%d_%d" % (i, pair))
-            nc.gpsimd.tensor_tensor(out=factor[:], in0=inverse[:], in1=signs[:], op=ALU.mult)
+            factor = keep.tile([P, 1], F32, name="factor%d_%d" % (i, pair))
+            mult = nc.vector.tensor_tensor if i in (3,) else nc.gpsimd.tensor_tensor
+            mult(out=factor[:], in0=inverse[:, 1:2], in1=signs[:, 1:2], op=ALU.mult)
+            inverses[i, pair] = inverse
             factors[i, pair] = factor
 
         def scale_first(i, pair):
@@ -462,7 +468,7 @@ def tile_refphi4flashdiffattention_pa_kernel(
                 out=scaled[:],
                 in_=o_banks[i, pair][:, 0, :],
                 func=FUNC.Copy,
-                scale=factors[i, pair][:, 0:1],
+                scale=inverses[i, pair][:, 0:1],
             )
             firsts[i, pair] = scaled
 
@@ -471,7 +477,7 @@ def tile_refphi4flashdiffattention_pa_kernel(
             nc.vector.scalar_tensor_tensor(
                 out=x[:, 0:PAIR_DIM],
                 in0=o_banks[i, pair][:, 1, :],
-                scalar=factors[i, pair][:, 1:2],
+                scalar=factors[i, pair][:, 0:1],
                 in1=firsts[i, pair][:],
                 op0=ALU.mult,
                 op1=ALU.add,
@@ -552,7 +558,7 @@ def tile_refphi4flashdiffattention_pa_kernel(
         fns = dict(spread=spread_vectors, prod=lam_products, gain=scale_gain, dots=lam_dots, signs=lam_signs,
             rv0=lambda: regroup_values(0), rv1=lambda: regroup_values(1), qv0=lambda: quantise_values(0), qv1=lambda: quantise_values(1),
             p0=lambda: part_values(0), p1=lambda: part_values(1), p2=lambda: part_values(2), p4=lambda: part_values(4), p5=lambda: part_values(5), p6=lambda: part_values(6))
-        for nm, tk in [('spread',0),('prod',1),('gain',1),('rv0',0),('rv1',2),('dots',3),('signs',4),('qv0',3),('p2',3),('p1',3),('p0',3),('qv1',4),('p4',4),('p5',4),('p6',4)]:
+        for nm, tk in [('spread',0),('prod',1),('gain',1),('rv0',2),('rv1',3),('dots',3),('signs',4),('qv0',3),('p2',3),('p1',3),('p0',3),('qv1',4),('p4',4),('p5',4),('p6',4)]:
             ONCE.setdefault(tk, []).append(fns[nm])
 
         with tc.manual_schedule():

@@ -45,6 +45,11 @@ STEPS = [
 FLOPS = 2 * HEADS * (512 * 512 + 512 * 1024) * (DIM + PAIR_DIM)
 
 
+def key_order(columns, ordered):
+    pattern = "q (u p e) -> q u p e" if ordered else "q (p u e) -> q u p e"
+    return columns.rearrange(pattern, u=2, e=2)
+
+
 def partner(i):
     return 6 - i
 
@@ -131,7 +136,9 @@ def tile_refphi4flashdiffattention_pa_kernel(
             channel_multiplier=1,
         )
         mask_bf = keep.tile([P, P], BF16, name="mask_bf")
-        nc.vector.tensor_copy(out=mask_bf[:], in_=mask_f32[:])
+        nc.vector.tensor_copy(out=key_order(mask_bf[:], True), in_=key_order(mask_f32[:], False))
+        order_bf = keep.tile([P, P], BF16, name="order_bf")
+        nc.vector.tensor_copy(out=key_order(order_bf[:], True), in_=key_order(ident_bf[:], False))
         ident_f32 = keep.tile([P, P], F32, name="ident_f32")
         make_identity(nc, ident_f32[:])
         minus_one = keep.tile([P, 2], F32, name="minus_one")
@@ -259,10 +266,10 @@ def tile_refphi4flashdiffattention_pa_kernel(
             pool, tag = (ps_o, "o_bank") if j in (1, 3) else (ps_t, "t")
             k_bank = pool.tile([P, HEADS, P], BF16, name="k_bank", tag=tag)
             q_bank = pool.tile([P, HEADS, P], BF16, name="q_bank", tag=tag)
-            for bank, rows in ((k_bank, k_sb[j]), (q_bank, q_sb[j])):
+            for bank, rows, order in ((k_bank, k_sb[j], order_bf), (q_bank, q_sb[j], ident_bf)):
                 for h in range(HEADS):
                     nc.tensor.transpose(
-                        bank[:, h, :], rows[:, h * DIM : (h + 1) * DIM], ident_bf[:]
+                        bank[:, h, :], rows[:, h * DIM : (h + 1) * DIM], order[:]
                     )
             rows_ps[j] = (k_bank, q_bank)
 
@@ -369,9 +376,9 @@ def tile_refphi4flashdiffattention_pa_kernel(
                 nc.scalar.activation(
                     out=e_tiles[owner, h][
                         :, number, :, first // 2 : (first + width) // 2
-                    ].rearrange("q u (p e) -> q u p e", e=2),
+                    ].rearrange("q u (j w) -> q u j w", w=P // 2),
                     in_=bank[:, column : column + width].rearrange(
-                        "q (p u e) -> q u p e", u=2, e=2
+                        "q (j u w) -> q u j w", u=2, w=P // 2
                     ),
                     func=FUNC.Exp,
                     bias=shifts[n][:, index : index + 1],

@@ -89,8 +89,8 @@ def tile_refphi4flashdiffattention_pa_kernel(
         ps_t = stack.enter_context(tc.psum_pool(name="ps_t", bufs=2))
         ps_o = stack.enter_context(tc.psum_pool(name="ps_o", bufs=2))
 
-        table = keep.tile([P, 1], F32, name="table")
-        nc.vector.memset(table[:], 0.0)
+        zero = keep.tile([P, 1], F32, name="zero")
+        nc.vector.memset(zero[:], 0.0)
         first_row = keep.tile([P, 4 * DIM + PAIR_DIM], BF16, name="first_row")
         nc.vector.memset(first_row[:], 0.0)
         for slot, vector in enumerate((lambda_q1, lambda_q2, lambda_k1, lambda_k2)):
@@ -99,7 +99,8 @@ def tile_refphi4flashdiffattention_pa_kernel(
             )
         nc.scalar.dma_start(out=first_row[0:1, 4 * DIM :], in_=subln_weight.unsqueeze(0))
 
-        nc.scalar.activation(out=table[:], in_=table[:], func=FUNC.Exp)
+        exp_one = keep.tile([P, 1], F32, name="exp_one")
+        nc.scalar.activation(out=exp_one[:], in_=zero[:], func=FUNC.Exp)
 
         q_sb = [keep.tile([P, ROW], BF16, name="q_sb%d" % j) for j in range(Q_TILES)]
         k_sb = [keep.tile([P, ROW], BF16, name="k_sb%d" % j) for j in range(Q_TILES)]
@@ -149,9 +150,9 @@ def tile_refphi4flashdiffattention_pa_kernel(
         x_tiles = []
         for index in range(X_TILES):
             x_tile = keep.tile([P, PAIR_DIM + 1], F32, name="x_tile%d" % index)
-            nc.gpsimd.tensor_scalar(
+            nc.vector.tensor_scalar(
                 out=x_tile[:, PAIR_DIM : PAIR_DIM + 1],
-                in0=minus_half[:],
+                in0=zero[:],
                 scalar1=0.0,
                 scalar2=math.sqrt(PAIR_DIM * EPS),
                 op0=ALU.mult,
@@ -161,7 +162,7 @@ def tile_refphi4flashdiffattention_pa_kernel(
 
         ones = keep.tile([P, P], BF16, name="ones")
         nc.vector.memset(ones[:], 1.0)
-        lam_in = keep.tile([P, 4, DIM], F32, name="lam_in")
+        lam_in = keep.tile([P, 2, DIM], F32, name="lam_in")
         products = keep.tile([P, 2, DIM], F32, name="products")
         unread = keep.tile([P, 2, DIM], F32, name="unread")
         dots = keep.tile([P, 2], F32, name="dots")
@@ -189,9 +190,10 @@ def tile_refphi4flashdiffattention_pa_kernel(
             spread_banks["weight"] = weight_bank
 
         def lam_products():
-            nc.scalar.copy(out=lam_in[:], in_=spread_banks["lam"][:])
-            nc.gpsimd.tensor_tensor(
-                out=products[:], in0=lam_in[:, 0:2, :], in1=lam_in[:, 2:4, :], op=ALU.mult
+            bank = spread_banks["lam"]
+            nc.scalar.copy(out=lam_in[:], in_=bank[:, 2:4, :])
+            nc.vector.tensor_tensor(
+                out=products[:], in0=bank[:, 0:2, :], in1=lam_in[:], op=ALU.mult
             )
 
         def scale_gain():
@@ -230,7 +232,7 @@ def tile_refphi4flashdiffattention_pa_kernel(
         v_part = {}
         for i in (2, 4, 1, 5, 0, 6):
             v_part[i] = keep.tile([P, ROW], U32, name="v_part%d" % i, align_bytes=64)
-            nc.gpsimd.memset(v_part[i][:], 0)
+            nc.vector.memset(v_part[i][:], 0)
 
         def regroup_values(g):
             w = 160

@@ -89,29 +89,35 @@ def tile_refphi4flashdiffattention_pa_kernel(
         ps_t = stack.enter_context(tc.psum_pool(name="ps_t", bufs=2))
         ps_o = stack.enter_context(tc.psum_pool(name="ps_o", bufs=2))
 
+        stack.enter_context(tc.manual_schedule())
+
         zero = keep.tile([P, 1], F32, name="zero")
         nc.vector.memset(zero[:], 0.0)
         first_row = keep.tile([P, 4 * DIM + PAIR_DIM], BF16, name="first_row")
-        nc.vector.memset(first_row[:], 0.0)
-        for slot, vector in enumerate((lambda_q1, lambda_q2, lambda_k1, lambda_k2)):
-            nc.scalar.dma_start(
-                out=first_row[0:1, slot * DIM : (slot + 1) * DIM], in_=vector.unsqueeze(0)
-            )
-        nc.scalar.dma_start(out=first_row[0:1, 4 * DIM :], in_=subln_weight.unsqueeze(0))
+        nc.vector.memset(first_row[:].bitcast(U32), 0)
 
         exp_one = keep.tile([P, 1], F32, name="exp_one")
         nc.scalar.activation(out=exp_one[:], in_=zero[:], func=FUNC.Exp)
 
-        q_sb = [keep.tile([P, ROW], BF16, name="q_sb%d" % j) for j in range(Q_TILES)]
-        k_sb = [keep.tile([P, ROW], BF16, name="k_sb%d" % j) for j in range(Q_TILES)]
+        q_sb = {}
+        k_sb = {}
         v_raw = [keep.tile([P, PACK, ROW], BF16, name="v_raw%d" % g) for g in range(PASSES)]
 
-        def load_rows(j):
-            nc.sync.dma_start(out=k_sb[j][:], in_=k_rows[:, j, :])
-            nc.sync.dma_start(out=q_sb[j][:], in_=q_rows[:, j, :])
+        def load_rows(first, last):
+            for rows, tiles, name in ((k_rows, k_sb, "k"), (q_rows, q_sb, "q")):
+                tile = keep.tile([P, last - first, ROW], BF16, name="%s_sb%d" % (name, first))
+                nc.sync.dma_start(out=tile[:], in_=rows[:, first:last, :])
+                for j in range(first, last):
+                    tiles[j] = tile[:, j - first, :]
 
-        for j in range(5):
-            load_rows(j)
+        load_rows(0, 1)
+        load_rows(1, 3)
+        load_rows(3, 5)
+        for slot, vector in enumerate((lambda_q1, lambda_q2, lambda_k1, lambda_k2)):
+            nc.sync.dma_start(
+                out=first_row[0:1, slot * DIM : (slot + 1) * DIM], in_=vector.unsqueeze(0)
+            )
+        nc.sync.dma_start(out=first_row[0:1, 4 * DIM :], in_=subln_weight.unsqueeze(0))
         nc.sync.dma_start(out=v_raw[0][:].rearrange("p t c -> p (t c)"), in_=v_pass_rows[:, 0, :])
         for b in range(TILES_PER_PASS):
             nc.sync.dma_start(
@@ -120,8 +126,7 @@ def tile_refphi4flashdiffattention_pa_kernel(
                 ),
                 in_=v_tile_rows[:, Q_TILES - 1 - b, :],
             )
-        for j in range(5, Q_TILES):
-            load_rows(j)
+        load_rows(5, 8)
 
         ident_bf = keep.tile([P, P], BF16, name="ident_bf")
         make_identity(nc, ident_bf[:])
@@ -142,9 +147,7 @@ def tile_refphi4flashdiffattention_pa_kernel(
         nc.vector.tensor_copy(out=key_order(order_bf[:], True), in_=key_order(ident_bf[:], False))
         ident_f32 = keep.tile([P, P], F32, name="ident_f32")
         make_identity(nc, ident_f32[:])
-        minus_one = keep.tile([P, 2], F32, name="minus_one")
-        nc.gpsimd.memset(minus_one[:], -1.0)
-        minus_half = keep.tile([P, 1], F32, name="minus_half")
+        minus_half = keep.tile([P, 2], F32, name="minus_half")
         nc.gpsimd.memset(minus_half[:], -0.5)
 
         x_tiles = []
@@ -167,9 +170,7 @@ def tile_refphi4flashdiffattention_pa_kernel(
         unread = keep.tile([P, 2, DIM], F32, name="unread")
         dots = keep.tile([P, 2], F32, name="dots")
         powers = keep.tile([P, 2], F32, name="powers")
-        difference = keep.tile([P, 1], F32, name="difference")
-        signs = keep.tile([P, 2], F32, name="signs")
-        nc.gpsimd.memset(signs[:, 0:1], 1.0)
+        minus_lam = keep.tile([P, 1], F32, name="minus_lam")
         gain = keep.tile([P, PAIR_DIM], F32, name="gain")
         spread_banks = {}
 
@@ -214,10 +215,14 @@ def tile_refphi4flashdiffattention_pa_kernel(
 
         def lam_signs():
             nc.scalar.activation(out=powers[:], in_=dots[:], func=FUNC.Exp)
-            nc.gpsimd.tensor_tensor(
-                out=difference[:], in0=powers[:, 1:2], in1=powers[:, 0:1], op=ALU.subtract
+            nc.vector.tensor_scalar(
+                out=minus_lam[:],
+                in0=powers[:, 1:2],
+                scalar1=powers[:, 0:1],
+                scalar2=LAMBDA_INIT,
+                op0=ALU.subtract,
+                op1=ALU.subtract,
             )
-            nc.gpsimd.tensor_scalar_add(out=signs[:, 1:2], in0=difference[:], scalar1=-LAMBDA_INIT)
 
         v_grouped = [
             keep.tile([P, ROW * PACK], BF16, name="v_grouped%d" % g, align_bytes=64)
@@ -232,6 +237,8 @@ def tile_refphi4flashdiffattention_pa_kernel(
         v_part = {}
         for i in (2, 4, 1, 5, 0, 6):
             v_part[i] = keep.tile([P, ROW], U32, name="v_part%d" % i, align_bytes=64)
+
+        def clear_part(i):
             nc.vector.memset(v_part[i][:], 0)
 
         def regroup_values(g):
@@ -292,7 +299,19 @@ def tile_refphi4flashdiffattention_pa_kernel(
         s_banks = {}
         tops = {}
         shifts = {}
-        row_sums = {}
+        totals = {}
+        partial_sums = {}
+        inverses = {}
+        factors = {}
+        for i in (4, 5, 6, 7, 3):
+            for pair in range(PAIRS):
+                columns = 4 if shares(i) else 2
+                suffix = "%d_%d" % (i, pair)
+                totals[i, pair] = keep.tile([P, columns], F32, name="totals" + suffix)
+                inverses[i, pair] = keep.tile([P, columns], F32, name="inverses" + suffix)
+                factors[i, pair] = keep.tile([P, columns // 2], F32, name="factors" + suffix)
+                if len(segments(i)) == 2:
+                    partial_sums[i, pair] = keep.tile([P, 2, 2], F32, name="partial" + suffix)
         e_banks = {}
         e_grouped = {}
         e_codes = {}
@@ -369,11 +388,12 @@ def tile_refphi4flashdiffattention_pa_kernel(
             parts = segments(i)
             for bank, column, h, s in s_banks[n]:
                 pair, half = divmod(h, 2)
-                if (i, pair) not in row_sums:
-                    row_sums[i, pair] = keep.tile(
-                        [P, 2, len(parts)], F32, name="row_sum%d_%d" % (i, pair)
-                    )
                 g, first, width, diagonal, owner, number = parts[s]
+                if len(parts) == 2:
+                    row_sum = partial_sums[i, pair][:, half, s : s + 1]
+                else:
+                    column_of_sum = half if i == owner else 2 + half
+                    row_sum = totals[owner, pair][:, column_of_sum : column_of_sum + 1]
                 index = h - heads[0]
                 nc.scalar.activation(
                     out=e_tiles[owner, h][
@@ -385,7 +405,7 @@ def tile_refphi4flashdiffattention_pa_kernel(
                     func=FUNC.Exp,
                     bias=shifts[n][:, index : index + 1],
                     scale=SCALE,
-                    accum_out=row_sums[i, pair][:, half, s : s + 1],
+                    accum_out=row_sum,
                 )
 
         def turn(n):
@@ -447,46 +467,48 @@ def tile_refphi4flashdiffattention_pa_kernel(
                     low = partner(i)
                     attend(low, pair, half, c - 1 + half, [(1, v_part[low], v_scales[0])])
 
-        factors = {}
-        inverses = {}
         firsts = {}
         xs = {}
+        sums_sq = {}
         rstds = {}
 
-        def weigh(i, pair):
-            sums = row_sums[i, pair]
-            total = sums[:, :, 0]
+        def side(i):
+            return (partner(i), 1) if i < 3 else (i, 0)
+
+        def add_sums(i, pair):
             if len(segments(i)) == 2:
-                added = small.tile([P, 2], F32, name="added")
-                nc.gpsimd.tensor_tensor(out=added[:], in0=sums[:, :, 0], in1=sums[:, :, 1], op=ALU.add)
-                total = added[:]
-            inverse = keep.tile([P, 2], F32, name="inverse%d_%d" % (i, pair))
-            if i in (3,):
-                nc.vector.reciprocal(out=inverse[:], in_=total)
-            else:
-                nc.gpsimd.tensor_tensor(out=inverse[:], in0=total, in1=minus_one[:], op=ALU.pow)
-            factor = keep.tile([P, 1], F32, name="factor%d_%d" % (i, pair))
-            mult = nc.vector.tensor_tensor if i in (3,) else nc.gpsimd.tensor_tensor
-            mult(out=factor[:], in0=inverse[:, 1:2], in1=signs[:, 1:2], op=ALU.mult)
-            inverses[i, pair] = inverse
-            factors[i, pair] = factor
+                nc.vector.tensor_reduce(
+                    out=totals[i, pair][:, 0:2], in_=partial_sums[i, pair][:], axis=AXIS.X, op=ALU.add
+                )
+
+        def invert_sums(i, pair):
+            nc.vector.reciprocal(out=inverses[i, pair][:], in_=totals[i, pair][:])
+
+        def weigh(i, pair):
+            nc.vector.tensor_scalar_mul(
+                out=factors[i, pair][:],
+                in0=inverses[i, pair][:].rearrange("p (t h) -> p t h", h=2)[:, :, 1],
+                scalar1=minus_lam[:, 0:1],
+            )
 
         def scale_first(i, pair):
+            owner, place = side(i)
             scaled = work.tile([P, PAIR_DIM], F32, name="scaled")
             nc.scalar.activation(
                 out=scaled[:],
                 in_=o_banks[i, pair][:, 0, :],
                 func=FUNC.Copy,
-                scale=inverses[i, pair][:, 0:1],
+                scale=inverses[owner, pair][:, 2 * place : 2 * place + 1],
             )
             firsts[i, pair] = scaled
 
         def combine(i, pair):
+            owner, place = side(i)
             x = x_tiles[len(xs) % X_TILES]
             nc.vector.scalar_tensor_tensor(
                 out=x[:, 0:PAIR_DIM],
                 in0=o_banks[i, pair][:, 1, :],
-                scalar=factors[i, pair][:, 0:1],
+                scalar=factors[owner, pair][:, place : place + 1],
                 in1=firsts[i, pair][:],
                 op0=ALU.mult,
                 op1=ALU.add,
@@ -494,28 +516,38 @@ def tile_refphi4flashdiffattention_pa_kernel(
             xs[i, pair] = x
 
         def measure(i, pair):
+            owner, place = side(i)
+            if place == 0:
+                sums_sq[i, pair] = small.tile([P, 2], F32, name="sum_sq")
             squares = work.tile([P, PAIR_DIM + 1], F32, name="squares")
-            sum_sq = small.tile([P, 1], F32, name="sum_sq")
+            sum_sq = sums_sq[owner, pair][:, place : place + 1]
             x = xs[i, pair][:]
-            if i in (0, 1, 2):
+            if i in ():
                 nc.vector.scalar_tensor_tensor(
                     out=squares[:], in0=x, scalar=1.0, in1=x, op0=ALU.mult, op1=ALU.mult,
-                    accum_out=sum_sq[:],
+                    accum_out=sum_sq,
                 )
             else:
-                nc.scalar.activation(
-                    out=squares[:], in_=x, func=FUNC.Square, accum_out=sum_sq[:]
-                )
-            rstd = small.tile([P, 1], F32, name="rstd")
-            nc.gpsimd.tensor_tensor(out=rstd[:], in0=sum_sq[:], in1=minus_half[:], op=ALU.pow)
+                nc.scalar.activation(out=squares[:], in_=x, func=FUNC.Square, accum_out=sum_sq)
+
+        def root(i, pair):
+            count = 2 if shares(i) else 1
+            rstd = small.tile([P, 2], F32, name="rstd")
+            nc.gpsimd.tensor_tensor(
+                out=rstd[:, 0:count],
+                in0=sums_sq[i, pair][:, 0:count],
+                in1=minus_half[:, 0:count],
+                op=ALU.pow,
+            )
             rstds[i, pair] = rstd
 
         def finish(i, pair):
+            owner, place = side(i)
             y = work.tile([P, PAIR_DIM], F32, name="y")
             nc.vector.scalar_tensor_tensor(
                 out=y[:],
                 in0=xs[i, pair][:, 0:PAIR_DIM],
-                scalar=rstds[i, pair][:, 0:1],
+                scalar=rstds[owner, pair][:, place : place + 1],
                 in1=gain[:],
                 op0=ALU.mult,
                 op1=ALU.mult,
@@ -538,20 +570,27 @@ def tile_refphi4flashdiffattention_pa_kernel(
                 if shares(i):
                     stage(partner(i), h // 2)
 
-        ROWS = {-4:(0,),-3:(1,),-2:(2,),-1:(3,),0:(4,),4:(5,),7:(6,),11:(7,)}
+        def run_close(stage, c):
+            if closes(c) and STEPS[c][1][0] % 2 == 1:
+                stage(STEPS[c][0], STEPS[c][1][0] // 2)
+
+        ROWS = {-4:(0,),-2:(1,2),0:(3,4),4:(5,),7:(6,),11:(7,)}
 
         def tick(n):
             run(exponent, n)
             run(regroup, n - 1, closing=True)
             run_pair(scale_first, n - 3)
-            run_pair(lambda i, p: measure(i, p) if i not in (0, 1, 2) else None, n - 5)
+            run_pair(lambda i, p: measure(i, p) if i not in () else None, n - 5)
             run(row_tops, n + 1)
+            run_close(add_sums, n - 1)
             run(quantise, n - 2, closing=True)
+            run_close(invert_sums, n - 1)
             run_pair(combine, n - 4)
             run(shift, n + 1)
-            run_pair(lambda i, p: measure(i, p) if i in (0, 1, 2) else None, n - 5)
+            run_close(weigh, n - 1)
+            run_pair(lambda i, p: measure(i, p) if i in () else None, n - 5)
             run_pair(finish, n - 7)
-            run_pair(weigh, n - 1)
+            run_close(root, n - 5)
             for j in ROWS.get(n - 1, ()):
                 copy_rows(j)
             run(scores, n + 2)
@@ -566,10 +605,10 @@ def tile_refphi4flashdiffattention_pa_kernel(
         ONCE = {}
         fns = dict(spread=spread_vectors, prod=lam_products, gain=scale_gain, dots=lam_dots, signs=lam_signs,
             rv0=lambda: regroup_values(0), rv1=lambda: regroup_values(1), qv0=lambda: quantise_values(0), qv1=lambda: quantise_values(1),
-            p0=lambda: part_values(0), p1=lambda: part_values(1), p2=lambda: part_values(2), p4=lambda: part_values(4), p5=lambda: part_values(5), p6=lambda: part_values(6))
-        for nm, tk in [('spread',0),('prod',1),('gain',1),('rv0',2),('rv1',3),('dots',3),('signs',4),('qv0',3),('p2',3),('p1',3),('p0',3),('qv1',4),('p4',4),('p5',4),('p6',4)]:
+            p0=lambda: part_values(0), p1=lambda: part_values(1), p2=lambda: part_values(2), p4=lambda: part_values(4), p5=lambda: part_values(5), c24=lambda: (clear_part(2), clear_part(4)), c15=lambda: (clear_part(1), clear_part(5)), c06=lambda: (clear_part(0), clear_part(6)), p6=lambda: part_values(6))
+        for nm, tk in [('c24',-6),('c15',-2),('c06',1),('spread',0),('prod',1),('gain',1),('rv0',2),('rv1',3),('dots',3),('signs',4),('qv0',3),('p2',3),('p1',3),('p0',3),('qv1',4),('p4',4),('p5',4),('p6',4)]:
             ONCE.setdefault(tk, []).append(fns[nm])
 
-        with tc.manual_schedule():
+        if True:
             for n in range(-6, len(STEPS) + 7 + 1):
                 tick(n)

@@ -32,9 +32,9 @@ SCALE = 1.0 / math.sqrt(DIM)
 LAMBDA_INIT = 0.8 - 0.6 * math.exp(-0.3 * 12)
 NEG_INF = -1e30
 EPS = 1e-5
-X_TILES = 6
+X_TILES = 8
 
-TILE_ORDER = (0, 2, 4, 1, 5, 6, 7, 3)
+TILE_ORDER = (0, 1, 2, 4, 5, 6, 7, 3)
 TOGETHER = {0: 4, 1: 2, 2: 2}
 STEPS = [
     (i, tuple(range(h, h + TOGETHER.get(i, 1))))
@@ -91,13 +91,13 @@ def tile_refphi4flashdiffattention_pa_kernel(
 
         stack.enter_context(tc.manual_schedule())
 
-        zero = keep.tile([P, 1], F32, name="zero")
+        zero = keep.tile([P, X_TILES], F32, name="zero")
         nc.vector.memset(zero[:], 0.0)
         first_row = keep.tile([P, 4 * DIM + PAIR_DIM], BF16, name="first_row")
         nc.vector.memset(first_row[:].bitcast(U32), 0)
 
         exp_one = keep.tile([P, 1], F32, name="exp_one")
-        nc.scalar.activation(out=exp_one[:], in_=zero[:], func=FUNC.Exp)
+        nc.scalar.activation(out=exp_one[:], in_=zero[:, 0:1], func=FUNC.Exp)
 
         q_sb = {}
         k_sb = {}
@@ -150,18 +150,16 @@ def tile_refphi4flashdiffattention_pa_kernel(
         minus_half = keep.tile([P, 2], F32, name="minus_half")
         nc.gpsimd.memset(minus_half[:], -0.5)
 
-        x_tiles = []
-        for index in range(X_TILES):
-            x_tile = keep.tile([P, PAIR_DIM + 1], F32, name="x_tile%d" % index)
-            nc.vector.tensor_scalar(
-                out=x_tile[:, PAIR_DIM : PAIR_DIM + 1],
-                in0=zero[:],
-                scalar1=0.0,
-                scalar2=math.sqrt(PAIR_DIM * EPS),
-                op0=ALU.mult,
-                op1=ALU.add,
-            )
-            x_tiles.append(x_tile)
+        x_all = keep.tile([P, X_TILES, PAIR_DIM + 1], F32, name="x_all")
+        nc.vector.tensor_scalar(
+            out=x_all[:, :, PAIR_DIM],
+            in0=zero[:],
+            scalar1=0.0,
+            scalar2=math.sqrt(PAIR_DIM * EPS),
+            op0=ALU.mult,
+            op1=ALU.add,
+        )
+        x_tiles = [x_all[:, index, :] for index in range(X_TILES)]
 
         ones = keep.tile([P, P], BF16, name="ones")
         nc.vector.memset(ones[:], 1.0)
@@ -238,8 +236,18 @@ def tile_refphi4flashdiffattention_pa_kernel(
         for i in (2, 4, 1, 5, 0, 6):
             v_part[i] = keep.tile([P, ROW], U32, name="v_part%d" % i, align_bytes=64)
 
+        no_codes = keep.tile([P, ROW], U32, name="no_codes", align_bytes=64)
+        nc.vector.memset(no_codes[:], 0)
+
+        def part_rows(i):
+            own = (i + 1) * TILE_PARTS if i < TILES_PER_PASS else (Q_TILES - 1 - i) * TILE_PARTS
+            return (slice(0, own), slice(own, P)) if i < TILES_PER_PASS else (slice(own, P), slice(0, own))
+
         def clear_part(i):
-            nc.vector.memset(v_part[i][:], 0)
+            rest = part_rows(i)[1]
+            nc.sync.dma_start(
+                out=v_part[i][rest, :].bitcast(I32), in_=no_codes[rest, :].bitcast(I32)
+            )
 
         def regroup_values(g):
             w = 160
@@ -267,28 +275,51 @@ def tile_refphi4flashdiffattention_pa_kernel(
                 out=v_part[i][first:last, :].bitcast(I32), in_=v_codes[g][first:last, :].bitcast(I32)
             )
 
-        q_turned = [keep.tile([P, HEADS, P], BF16, name="q_turned%d" % j) for j in range(Q_TILES)]
-        k_turned = [keep.tile([P, HEADS, K_PASS], BF16, name="k_turned%d" % g) for g in range(PASSES)]
+        q_turned = keep.tile([P, Q_TILES, HEADS, P], BF16, name="q_turned")
+        k_turned = [
+            keep.tile([P, HEADS, TILES_PER_PASS, P], BF16, name="k_turned%d" % g)
+            for g in range(PASSES)
+        ]
         rows_ps = {}
 
-        def turn_rows(j):
-            pool, tag = (ps_o, "o_bank") if j in (1, 3) else (ps_t, "t")
-            k_bank = pool.tile([P, HEADS, P], BF16, name="k_bank", tag=tag)
-            q_bank = pool.tile([P, HEADS, P], BF16, name="q_bank", tag=tag)
-            for bank, rows, order in ((k_bank, k_sb[j], order_bf), (q_bank, q_sb[j], ident_bf)):
-                for h in range(HEADS):
-                    nc.tensor.transpose(
-                        bank[:, h, :], rows[:, h * DIM : (h + 1) * DIM], order[:]
-                    )
-            rows_ps[j] = (k_bank, q_bank)
+        def turn_rows(first, last):
+            where = 'totot111'[first]
+            count = last - first
+            if where == '1':
+                both = ps_t.tile([P, 2, HEADS, P], BF16, name="both_bank", tag="t")
+                banks = (both[:, 0:1, :, :], both[:, 1:2, :, :])
+            else:
+                pool, tag = (ps_o, "o_bank") if where == 'o' else (ps_t, "t")
+                k_bank = pool.tile([P, count, HEADS, P], BF16, name="k_bank", tag=tag)
+                q_bank = pool.tile([P, count, HEADS, P], BF16, name="q_bank", tag=tag)
+                banks = (k_bank[:], q_bank[:])
+            for bank, rows, order in ((banks[0], k_sb, order_bf), (banks[1], q_sb, ident_bf)):
+                for j in range(first, last):
+                    for h in range(HEADS):
+                        nc.tensor.transpose(
+                            bank[:, j - first, h, :], rows[j][:, h * DIM : (h + 1) * DIM], order[:]
+                        )
+            rows_ps[first] = banks
 
-        def copy_rows(j):
-            g = j // TILES_PER_PASS
-            t = j if g == 0 else Q_TILES - 1 - j
-            copy_q = nc.scalar.copy if j < 5 else nc.vector.tensor_copy
-            k_bank, q_bank = rows_ps[j]
-            nc.vector.tensor_copy(out=k_turned[g][:, :, t * P : (t + 1) * P], in_=k_bank[:])
-            copy_q(out=q_turned[j][:], in_=q_bank[:])
+        def copy_rows(first, last):
+            k_bank, q_bank = rows_ps[first]
+            cp = {'S': nc.scalar.copy, 'V': nc.vector.tensor_copy}
+            ck, cq = cp['VVVVVVVV'[first]], cp['SSSSSVVV'[first]]
+            j = first
+            while j < last:
+                g = j // TILES_PER_PASS
+                stop = min(last, (g + 1) * TILES_PER_PASS)
+                place = j - g * TILES_PER_PASS
+                if g == 1:
+                    for i in range(j, stop):
+                        ck(out=k_turned[1][:, :, Q_TILES - 1 - i, :], in_=k_bank[:, i - first, :, :])
+                else:
+                    ck(
+                        out=k_turned[0][:, :, place : place + stop - j, :].rearrange("p h j c -> p j h c"),
+                        in_=k_bank[:, j - first : stop - first, :, :],
+                    )
+                j = stop
+            cq(out=q_turned[:, first:last, :, :], in_=q_bank)
 
         e_tiles = {}
         for i in (4, 5, 6, 7, 3):
@@ -330,8 +361,10 @@ def tile_refphi4flashdiffattention_pa_kernel(
                         column = 0
                     nc.tensor.matmul(
                         out=bank[:, column : column + width],
-                        lhsT=q_turned[i][:, h, :],
-                        rhs=k_turned[g][:, h, first : first + width],
+                        lhsT=q_turned[:, i, h, :],
+                        rhs=k_turned[g][:, h, first // P : (first + width) // P, :].rearrange(
+                            "p j c -> p (j c)"
+                        ),
                         start=True,
                         stop=diagonal is None,
                     )
@@ -369,7 +402,7 @@ def tile_refphi4flashdiffattention_pa_kernel(
             i, heads = STEPS[n]
             bias = small.tile([P, HEADS], F32, name="bias")
             if len(segments(i)) == 2:
-                nc.vector.tensor_scalar(
+                (nc.gpsimd if True else nc.vector).tensor_scalar(
                     out=bias[:, 0:1],
                     in0=tops[n][:, 0:1],
                     scalar1=tops[n][:, 1:2],
@@ -378,9 +411,15 @@ def tile_refphi4flashdiffattention_pa_kernel(
                     op1=ALU.mult,
                 )
             else:
-                nc.vector.tensor_scalar_mul(
-                    out=bias[:, 0 : len(heads)], in0=tops[n][:, 0 : len(heads)], scalar1=-SCALE
-                )
+                if True:
+                    nc.gpsimd.tensor_scalar(
+                        out=bias[:, 0 : len(heads)], in0=tops[n][:, 0 : len(heads)],
+                        scalar1=-SCALE, scalar2=0.0, op0=ALU.mult, op1=ALU.add,
+                    )
+                else:
+                    nc.vector.tensor_scalar_mul(
+                        out=bias[:, 0 : len(heads)], in0=tops[n][:, 0 : len(heads)], scalar1=-SCALE
+                    )
             shifts[n] = bias
 
         def exponent(n):
@@ -437,35 +476,31 @@ def tile_refphi4flashdiffattention_pa_kernel(
             e_codes[n] = codes
             e_scales[n] = scales
 
-        def attend(i, pair, half, n, passes):
-            if half == 0:
-                o_banks[i, pair] = ps_o.tile([P, 2, PAIR_DIM], F32, name="o_bank")
-            features = slice(pair * PAIR_DIM, (pair + 1) * PAIR_DIM)
-            for index, (number, codes, scales) in enumerate(passes):
-                queries = slice(number * P, (number + 1) * P)
-                nc.tensor.matmul_mx(
-                    out=o_banks[i, pair][:, half, :],
-                    lhsT=e_codes[n][:, queries].bitcast(FP8X4),
-                    lhsT_scale=e_scales[n][:, queries],
-                    rhs=codes[:, features].bitcast(FP8X4),
-                    rhs_scale=scales[:, features],
-                    start=(index == 0),
-                    stop=(index == len(passes) - 1),
-                )
-
-        def attend_pair(c):
-            i, (h,) = STEPS[c]
-            pair = h // 2
+        def attend(n):
+            i, (h,) = STEPS[n]
+            bank = ps_o.tile([P, 2, PAIR_DIM], F32, name="o_bank")
+            features = slice(h // 2 * PAIR_DIM, (h // 2 + 1) * PAIR_DIM)
             passes = [(0, v_codes[0], v_scales[0])]
             if i == 7:
                 passes.append((1, v_codes[1], v_scales[1]))
             if shares(i):
                 passes.append((1, v_part[i], v_scales[1]))
-            for half in range(2):
-                attend(i, pair, half, c - 1 + half, passes)
-                if shares(i):
-                    low = partner(i)
-                    attend(low, pair, half, c - 1 + half, [(1, v_part[low], v_scales[0])])
+            products = [passes]
+            if shares(i):
+                products.append([(1, v_part[partner(i)], v_scales[0])])
+            for place, passes in enumerate(products):
+                for index, (number, codes, scales) in enumerate(passes):
+                    queries = slice(number * P, (number + 1) * P)
+                    nc.tensor.matmul_mx(
+                        out=bank[:, place, :],
+                        lhsT=e_codes[n][:, queries].bitcast(FP8X4),
+                        lhsT_scale=e_scales[n][:, queries],
+                        rhs=codes[:, features].bitcast(FP8X4),
+                        rhs_scale=scales[:, features],
+                        start=(index == 0),
+                        stop=(index == len(passes) - 1),
+                    )
+            o_banks[i, h] = bank
 
         firsts = {}
         xs = {}
@@ -477,9 +512,15 @@ def tile_refphi4flashdiffattention_pa_kernel(
 
         def add_sums(i, pair):
             if len(segments(i)) == 2:
-                nc.vector.tensor_reduce(
-                    out=totals[i, pair][:, 0:2], in_=partial_sums[i, pair][:], axis=AXIS.X, op=ALU.add
-                )
+                parts = partial_sums[i, pair]
+                if False:
+                    nc.gpsimd.tensor_tensor(
+                        out=totals[i, pair][:, 0:2], in0=parts[:, :, 0], in1=parts[:, :, 1], op=ALU.add
+                    )
+                else:
+                    nc.vector.tensor_reduce(
+                        out=totals[i, pair][:, 0:2], in_=parts[:], axis=AXIS.X, op=ALU.add
+                    )
 
         def invert_sums(i, pair):
             nc.vector.reciprocal(out=inverses[i, pair][:], in_=totals[i, pair][:])
@@ -494,12 +535,19 @@ def tile_refphi4flashdiffattention_pa_kernel(
         def scale_first(i, pair):
             owner, place = side(i)
             scaled = work.tile([P, PAIR_DIM], F32, name="scaled")
-            nc.scalar.activation(
-                out=scaled[:],
-                in_=o_banks[i, pair][:, 0, :],
-                func=FUNC.Copy,
-                scale=inverses[owner, pair][:, 2 * place : 2 * place + 1],
-            )
+            if i in ():
+                nc.vector.tensor_scalar_mul(
+                    out=scaled[:],
+                    in0=o_banks[owner, 2 * pair][:, place, :],
+                    scalar1=inverses[owner, pair][:, 2 * place : 2 * place + 1],
+                )
+            else:
+                nc.scalar.activation(
+                    out=scaled[:],
+                    in_=o_banks[owner, 2 * pair][:, place, :],
+                    func=FUNC.Copy,
+                    scale=inverses[owner, pair][:, 2 * place : 2 * place + 1],
+                )
             firsts[i, pair] = scaled
 
         def combine(i, pair):
@@ -507,7 +555,7 @@ def tile_refphi4flashdiffattention_pa_kernel(
             x = x_tiles[len(xs) % X_TILES]
             nc.vector.scalar_tensor_tensor(
                 out=x[:, 0:PAIR_DIM],
-                in0=o_banks[i, pair][:, 1, :],
+                in0=o_banks[owner, 2 * pair + 1][:, place, :],
                 scalar=factors[owner, pair][:, place : place + 1],
                 in1=firsts[i, pair][:],
                 op0=ALU.mult,
@@ -517,11 +565,11 @@ def tile_refphi4flashdiffattention_pa_kernel(
 
         def measure(i, pair):
             owner, place = side(i)
-            if place == 0:
-                sums_sq[i, pair] = small.tile([P, 2], F32, name="sum_sq")
+            if (owner, pair) not in sums_sq:
+                sums_sq[owner, pair] = small.tile([P, 2], F32, name="sum_sq")
             squares = work.tile([P, PAIR_DIM + 1], F32, name="squares")
             sum_sq = sums_sq[owner, pair][:, place : place + 1]
-            x = xs[i, pair][:]
+            x = xs[i, pair]
             if i in ():
                 nc.vector.scalar_tensor_tensor(
                     out=squares[:], in0=x, scalar=1.0, in1=x, op0=ALU.mult, op1=ALU.mult,
@@ -541,17 +589,33 @@ def tile_refphi4flashdiffattention_pa_kernel(
             )
             rstds[i, pair] = rstd
 
+        gained = {}
+
+        def apply_gain(i, pair):
+            product = work.tile([P, PAIR_DIM], F32, name="product")
+            nc.gpsimd.tensor_tensor(
+                out=product[:], in0=xs[i, pair][:, 0:PAIR_DIM], in1=gain[:], op=ALU.mult
+            )
+            gained[i, pair] = product
+
         def finish(i, pair):
             owner, place = side(i)
             y = work.tile([P, PAIR_DIM], F32, name="y")
-            nc.vector.scalar_tensor_tensor(
-                out=y[:],
-                in0=xs[i, pair][:, 0:PAIR_DIM],
-                scalar=rstds[owner, pair][:, place : place + 1],
-                in1=gain[:],
-                op0=ALU.mult,
-                op1=ALU.mult,
-            )
+            rstd = rstds[owner, pair][:, place : place + 1]
+            if i in ():
+                nc.gpsimd.tensor_scalar(
+                    out=y[:], in0=gained[i, pair][:], scalar1=rstd, scalar2=1.0,
+                    op0=ALU.mult, op1=ALU.mult,
+                )
+            else:
+                nc.vector.scalar_tensor_tensor(
+                    out=y[:],
+                    in0=xs[i, pair][:, 0:PAIR_DIM],
+                    scalar=rstd,
+                    in1=gain[:],
+                    op0=ALU.mult,
+                    op1=ALU.mult,
+                )
             nc.sync.dma_start(
                 out=out_rows[:, i, pair * PAIR_DIM : (pair + 1) * PAIR_DIM], in_=y[:]
             )
@@ -574,41 +638,61 @@ def tile_refphi4flashdiffattention_pa_kernel(
             if closes(c) and STEPS[c][1][0] % 2 == 1:
                 stage(STEPS[c][0], STEPS[c][1][0] // 2)
 
-        ROWS = {-4:(0,),-2:(1,2),0:(3,4),4:(5,),7:(6,),11:(7,)}
+        def warm_up():
+            bank = ps_o.tile([P, P], F32, name="warm_bank", tag="o_bank")
+            for index in range(10):
+                nc.tensor.matmul(
+                    out=bank[:], lhsT=ident_bf[:], rhs=ident_bf[:], start=True, stop=True
+                )
+
+        ROWS = {-4: ((0, 1),), -2: ((1, 2),), 0: ((2, 3),), 1: ((3, 4),), 2: ((4, 5),), 5: ((5, 6),), 9: ((6, 7),), 13: ((7, 8),)}
 
         def tick(n):
             run(exponent, n)
             run(regroup, n - 1, closing=True)
-            run_pair(scale_first, n - 3)
-            run_pair(lambda i, p: measure(i, p) if i not in () else None, n - 5)
             run(row_tops, n + 1)
-            run_close(add_sums, n - 1)
+            if False:
+                run_close(invert_sums, n - 1)
+            if not False:
+                run_close(add_sums, n - 1)
             run(quantise, n - 2, closing=True)
-            run_close(invert_sums, n - 1)
-            run_pair(combine, n - 4)
-            run(shift, n + 1)
+            quantised = closes(n - 2)
+            if quantised or True:
+                run(shift, n + 1)
+            if True:
+                run_close(invert_sums, n - 1)
+            run_pair(lambda i, p: scale_first(i, p) if i in () else None, n - 3)
+            run_pair(combine, n - 3)
+            if not (quantised or True):
+                run(shift, n + 1)
             run_close(weigh, n - 1)
-            run_pair(lambda i, p: measure(i, p) if i in () else None, n - 5)
-            run_pair(finish, n - 7)
-            run_close(root, n - 5)
-            for j in ROWS.get(n - 1, ()):
-                copy_rows(j)
+            run_pair(lambda i, p: measure(i, p) if i in () else None, n - 4)
+            run_pair(lambda i, p: finish(i, p) if i not in () else None, n - 6)
+            run_pair(lambda i, p: scale_first(i, p) if i not in () else None, n - 2)
+            run_pair(lambda i, p: measure(i, p) if i not in () else None, n - 4)
+            if False:
+                run_close(add_sums, n - 1)
+            run_close(root, n - 4)
+            run_pair(lambda i, p: apply_gain(i, p) if i in () else None, n - 4)
+            run_pair(lambda i, p: finish(i, p) if i in () else None, n - 5)
+            for group in ROWS.get(n - 1, ()):
+                copy_rows(*group)
             run(scores, n + 2)
             run(turn, n, closing=True)
-            if closes(n - 2) and STEPS[n - 2][1][0] % 2 == 1:
-                attend_pair(n - 2)
-            for j in ROWS.get(n, ()):
-                turn_rows(j)
+            run(attend, n - 2, closing=True)
+            for group in ROWS.get(n, ()):
+                turn_rows(*group)
             for once in ONCE.get(n, []):
                 once()
 
         ONCE = {}
         fns = dict(spread=spread_vectors, prod=lam_products, gain=scale_gain, dots=lam_dots, signs=lam_signs,
             rv0=lambda: regroup_values(0), rv1=lambda: regroup_values(1), qv0=lambda: quantise_values(0), qv1=lambda: quantise_values(1),
-            p0=lambda: part_values(0), p1=lambda: part_values(1), p2=lambda: part_values(2), p4=lambda: part_values(4), p5=lambda: part_values(5), c24=lambda: (clear_part(2), clear_part(4)), c15=lambda: (clear_part(1), clear_part(5)), c06=lambda: (clear_part(0), clear_part(6)), p6=lambda: part_values(6))
-        for nm, tk in [('c24',-6),('c15',-2),('c06',1),('spread',0),('prod',1),('gain',1),('rv0',2),('rv1',3),('dots',3),('signs',4),('qv0',3),('p2',3),('p1',3),('p0',3),('qv1',4),('p4',4),('p5',4),('p6',4)]:
+            p0=lambda: part_values(0), p1=lambda: part_values(1), p2=lambda: part_values(2), p4=lambda: part_values(4), p5=lambda: part_values(5), c24=lambda: [clear_part(i) for i in (2, 4, 1, 5, 0, 6)], p6=lambda: part_values(6))
+        for nm, tk in [('c24',-6),('spread',0),('prod',1),('gain',1),('rv0',3),('rv1',4),('dots',4),('signs',5),('qv0',4),('p2',4),('p1',4),('p0',4),('qv1',5),('p4',5),('p5',5),('p6',5)]:
             ONCE.setdefault(tk, []).append(fns[nm])
 
-        if True:
-            for n in range(-6, len(STEPS) + 7 + 1):
-                tick(n)
+        if 10:
+            warm_up()
+        for n in range(-6, len(STEPS) + 6 + 1):
+            tick(n)

@@ -32,7 +32,7 @@ SCALE = 1.0 / math.sqrt(DIM)
 LAMBDA_INIT = 0.8 - 0.6 * math.exp(-0.3 * 12)
 NEG_INF = -1e30
 EPS = 1e-5
-X_TILES = 8
+X_TILES = 16
 
 TILE_ORDER = (0, 1, 2, 4, 5, 6, 7, 3)
 TOGETHER = {0: 4, 1: 2, 2: 2}
@@ -91,6 +91,8 @@ def tile_refphi4flashdiffattention_pa_kernel(
 
         stack.enter_context(tc.manual_schedule())
 
+        ones = keep.tile([P, P], BF16, name="ones")
+        nc.vector.memset(ones[:], 1.0)
         zero = keep.tile([P, X_TILES], F32, name="zero")
         nc.vector.memset(zero[:], 0.0)
         first_row = keep.tile([P, 4 * DIM + PAIR_DIM], BF16, name="first_row")
@@ -110,9 +112,8 @@ def tile_refphi4flashdiffattention_pa_kernel(
                 for j in range(first, last):
                     tiles[j] = tile[:, j - first, :]
 
-        load_rows(0, 1)
-        load_rows(1, 3)
-        load_rows(3, 5)
+        for first, last in ((0, 1), (1, 2), (2, 3), (3, 5)):
+            load_rows(first, last)
         for slot, vector in enumerate((lambda_q1, lambda_q2, lambda_k1, lambda_k2)):
             nc.sync.dma_start(
                 out=first_row[0:1, slot * DIM : (slot + 1) * DIM], in_=vector.unsqueeze(0)
@@ -161,8 +162,6 @@ def tile_refphi4flashdiffattention_pa_kernel(
         )
         x_tiles = [x_all[:, index, :] for index in range(X_TILES)]
 
-        ones = keep.tile([P, P], BF16, name="ones")
-        nc.vector.memset(ones[:], 1.0)
         lam_in = keep.tile([P, 2, DIM], F32, name="lam_in")
         products = keep.tile([P, 2, DIM], F32, name="products")
         unread = keep.tile([P, 2, DIM], F32, name="unread")
@@ -275,51 +274,25 @@ def tile_refphi4flashdiffattention_pa_kernel(
                 out=v_part[i][first:last, :].bitcast(I32), in_=v_codes[g][first:last, :].bitcast(I32)
             )
 
-        q_turned = keep.tile([P, Q_TILES, HEADS, P], BF16, name="q_turned")
-        k_turned = [
-            keep.tile([P, HEADS, TILES_PER_PASS, P], BF16, name="k_turned%d" % g)
-            for g in range(PASSES)
-        ]
+        turned = keep.tile([P, Q_TILES, 2, HEADS, P], BF16, name="turned")
+
+        def slot(j):
+            return j if j < TILES_PER_PASS else 3 * TILES_PER_PASS - 1 - j
+
         rows_ps = {}
 
-        def turn_rows(first, last):
-            where = 'totot111'[first]
-            count = last - first
-            if where == '1':
-                both = ps_t.tile([P, 2, HEADS, P], BF16, name="both_bank", tag="t")
-                banks = (both[:, 0:1, :, :], both[:, 1:2, :, :])
-            else:
-                pool, tag = (ps_o, "o_bank") if where == 'o' else (ps_t, "t")
-                k_bank = pool.tile([P, count, HEADS, P], BF16, name="k_bank", tag=tag)
-                q_bank = pool.tile([P, count, HEADS, P], BF16, name="q_bank", tag=tag)
-                banks = (k_bank[:], q_bank[:])
-            for bank, rows, order in ((banks[0], k_sb, order_bf), (banks[1], q_sb, ident_bf)):
-                for j in range(first, last):
-                    for h in range(HEADS):
-                        nc.tensor.transpose(
-                            bank[:, j - first, h, :], rows[j][:, h * DIM : (h + 1) * DIM], order[:]
-                        )
-            rows_ps[first] = banks
-
-        def copy_rows(first, last):
-            k_bank, q_bank = rows_ps[first]
-            cp = {'S': nc.scalar.copy, 'V': nc.vector.tensor_copy}
-            ck, cq = cp['VVVVVVVV'[first]], cp['SSSSSVVV'[first]]
-            j = first
-            while j < last:
-                g = j // TILES_PER_PASS
-                stop = min(last, (g + 1) * TILES_PER_PASS)
-                place = j - g * TILES_PER_PASS
-                if g == 1:
-                    for i in range(j, stop):
-                        ck(out=k_turned[1][:, :, Q_TILES - 1 - i, :], in_=k_bank[:, i - first, :, :])
-                else:
-                    ck(
-                        out=k_turned[0][:, :, place : place + stop - j, :].rearrange("p h j c -> p j h c"),
-                        in_=k_bank[:, j - first : stop - first, :, :],
+        def turn_rows(j):
+            pool, tag = (ps_o, "o_bank") if j in (1, 3) else (ps_t, "t")
+            bank = pool.tile([P, 2, HEADS, P], BF16, name="rows_bank", tag=tag)
+            for which, rows, order in ((0, k_sb, order_bf), (1, q_sb, ident_bf)):
+                for h in range(HEADS):
+                    nc.tensor.transpose(
+                        bank[:, which, h, :], rows[j][:, h * DIM : (h + 1) * DIM], order[:]
                     )
-                j = stop
-            cq(out=q_turned[:, first:last, :, :], in_=q_bank)
+            rows_ps[j] = bank
+
+        def copy_rows(j):
+            nc.vector.tensor_copy(out=turned[:, slot(j), :, :, :], in_=rows_ps[j][:])
 
         e_tiles = {}
         for i in (4, 5, 6, 7, 3):
@@ -360,11 +333,11 @@ def tile_refphi4flashdiffattention_pa_kernel(
                         bank = ps_s.tile([P, K_PASS], F32, name="s_bank")
                         column = 0
                     nc.tensor.matmul(
-                        out=bank[:, column : column + width],
-                        lhsT=q_turned[:, i, h, :],
-                        rhs=k_turned[g][:, h, first // P : (first + width) // P, :].rearrange(
-                            "p j c -> p (j c)"
-                        ),
+                        out=bank[:, column : column + width].rearrange("q (j c) -> q j c", c=P),
+                        lhsT=turned[:, slot(i), 1, h, :],
+                        rhs=turned[
+                            :, (g * K_PASS + first) // P : (g * K_PASS + first + width) // P, 0, h, :
+                        ],
                         start=True,
                         stop=diagonal is None,
                     )
@@ -638,14 +611,26 @@ def tile_refphi4flashdiffattention_pa_kernel(
             if closes(c) and STEPS[c][1][0] % 2 == 1:
                 stage(STEPS[c][0], STEPS[c][1][0] // 2)
 
+        def late_pair(stage, n, lag):
+            for extra in sorted(set([0] + list({}.values())), reverse=True):
+                c = n - lag - extra
+                if closes(c) and {}.get(STEPS[c][0], 0) == extra:
+                    run_pair(stage, c)
+
+        def late_close(stage, n, lag):
+            for extra in sorted(set([0] + list({}.values())), reverse=True):
+                c = n - lag - extra
+                if closes(c) and {}.get(STEPS[c][0], 0) == extra:
+                    run_close(stage, c)
+
         def warm_up():
             bank = ps_o.tile([P, P], F32, name="warm_bank", tag="o_bank")
-            for index in range(10):
+            for index in range(16):
                 nc.tensor.matmul(
-                    out=bank[:], lhsT=ident_bf[:], rhs=ident_bf[:], start=True, stop=True
+                    out=bank[:], lhsT=ones[:], rhs=ones[:], start=True, stop=True
                 )
 
-        ROWS = {-4: ((0, 1),), -2: ((1, 2),), 0: ((2, 3),), 1: ((3, 4),), 2: ((4, 5),), 5: ((5, 6),), 9: ((6, 7),), 13: ((7, 8),)}
+        ROWS = {-4: ((0, 1),), -3: ((1, 2),), -1: ((2, 3),), 0: ((3, 4),), 1: ((4, 5),), 5: ((5, 6),), 9: ((6, 7),), 13: ((7, 8),)}
 
         def tick(n):
             run(exponent, n)
@@ -666,22 +651,22 @@ def tile_refphi4flashdiffattention_pa_kernel(
             if not (quantised or True):
                 run(shift, n + 1)
             run_close(weigh, n - 1)
-            run_pair(lambda i, p: measure(i, p) if i in () else None, n - 4)
-            run_pair(lambda i, p: finish(i, p) if i not in () else None, n - 6)
+            late_pair(lambda i, p: measure(i, p) if i in () else None, n, 4)
+            late_pair(lambda i, p: finish(i, p) if i not in () else None, n, 6)
             run_pair(lambda i, p: scale_first(i, p) if i not in () else None, n - 2)
-            run_pair(lambda i, p: measure(i, p) if i not in () else None, n - 4)
+            late_pair(lambda i, p: measure(i, p) if i not in () else None, n, 4)
             if False:
                 run_close(add_sums, n - 1)
-            run_close(root, n - 4)
+            late_close(root, n, 4)
             run_pair(lambda i, p: apply_gain(i, p) if i in () else None, n - 4)
             run_pair(lambda i, p: finish(i, p) if i in () else None, n - 5)
             for group in ROWS.get(n - 1, ()):
-                copy_rows(*group)
+                copy_rows(group[0])
             run(scores, n + 2)
             run(turn, n, closing=True)
             run(attend, n - 2, closing=True)
             for group in ROWS.get(n, ()):
-                turn_rows(*group)
+                turn_rows(group[0])
             for once in ONCE.get(n, []):
                 once()
 
@@ -689,10 +674,10 @@ def tile_refphi4flashdiffattention_pa_kernel(
         fns = dict(spread=spread_vectors, prod=lam_products, gain=scale_gain, dots=lam_dots, signs=lam_signs,
             rv0=lambda: regroup_values(0), rv1=lambda: regroup_values(1), qv0=lambda: quantise_values(0), qv1=lambda: quantise_values(1),
             p0=lambda: part_values(0), p1=lambda: part_values(1), p2=lambda: part_values(2), p4=lambda: part_values(4), p5=lambda: part_values(5), c24=lambda: [clear_part(i) for i in (2, 4, 1, 5, 0, 6)], p6=lambda: part_values(6))
-        for nm, tk in [('c24',-6),('spread',0),('prod',1),('gain',1),('rv0',3),('rv1',4),('dots',4),('signs',5),('qv0',4),('p2',4),('p1',4),('p0',4),('qv1',5),('p4',5),('p5',5),('p6',5)]:
+        for nm, tk in [('c24',-6),('spread',1),('prod',2),('gain',2),('rv0',3),('rv1',4),('dots',4),('signs',5),('qv0',4),('p2',4),('p1',4),('p0',4),('qv1',5),('p4',5),('p5',5),('p6',5)]:
             ONCE.setdefault(tk, []).append(fns[nm])
 
-        if 10:
+        if 16:
             warm_up()
-        for n in range(-6, len(STEPS) + 6 + 1):
+        for n in range(-6, len(STEPS) + 6 + 12):
             tick(n)

@@ -283,16 +283,25 @@ def tile_refphi4flashdiffattention_pa_kernel(
 
         def turn_rows(j):
             pool, tag = (ps_o, "o_bank") if j in (1, 3) else (ps_t, "t")
-            bank = pool.tile([P, 2, HEADS, P], BF16, name="rows_bank", tag=tag)
+            banks = []
             for which, rows, order in ((0, k_sb, order_bf), (1, q_sb, ident_bf)):
+                if which == 0 or j in (0,):
+                    banks.append(pool.tile([P, 2, HEADS, P], BF16, name="rows_bank", tag=tag))
                 for h in range(HEADS):
                     nc.tensor.transpose(
-                        bank[:, which, h, :], rows[j][:, h * DIM : (h + 1) * DIM], order[:]
+                        banks[-1][:, which, h, :], rows[j][:, h * DIM : (h + 1) * DIM], order[:]
                     )
-            rows_ps[j] = bank
+            rows_ps[j] = banks
 
         def copy_rows(j):
-            nc.vector.tensor_copy(out=turned[:, slot(j), :, :, :], in_=rows_ps[j][:])
+            banks = rows_ps[j]
+            if len(banks) == 2:
+                for which, bank in enumerate(banks):
+                    nc.vector.tensor_copy(
+                        out=turned[:, slot(j), which, :, :], in_=bank[:, which, :, :]
+                    )
+            else:
+                nc.vector.tensor_copy(out=turned[:, slot(j), :, :, :], in_=banks[0][:])
 
         e_tiles = {}
         for i in (4, 5, 6, 7, 3):
@@ -375,7 +384,7 @@ def tile_refphi4flashdiffattention_pa_kernel(
             i, heads = STEPS[n]
             bias = small.tile([P, HEADS], F32, name="bias")
             if len(segments(i)) == 2:
-                (nc.gpsimd if True else nc.vector).tensor_scalar(
+                (nc.gpsimd if i in (0, 1, 2, 3, 4, 5, 6, 7) else nc.vector).tensor_scalar(
                     out=bias[:, 0:1],
                     in0=tops[n][:, 0:1],
                     scalar1=tops[n][:, 1:2],
@@ -384,7 +393,7 @@ def tile_refphi4flashdiffattention_pa_kernel(
                     op1=ALU.mult,
                 )
             else:
-                if True:
+                if i in (0, 1, 2, 3, 4, 5, 6, 7):
                     nc.gpsimd.tensor_scalar(
                         out=bias[:, 0 : len(heads)], in0=tops[n][:, 0 : len(heads)],
                         scalar1=-SCALE, scalar2=0.0, op0=ALU.mult, op1=ALU.add,
@@ -508,7 +517,7 @@ def tile_refphi4flashdiffattention_pa_kernel(
         def scale_first(i, pair):
             owner, place = side(i)
             scaled = work.tile([P, PAIR_DIM], F32, name="scaled")
-            if i in ():
+            if i in (2,):
                 nc.vector.tensor_scalar_mul(
                     out=scaled[:],
                     in0=o_banks[owner, 2 * pair][:, place, :],
@@ -612,20 +621,27 @@ def tile_refphi4flashdiffattention_pa_kernel(
                 stage(STEPS[c][0], STEPS[c][1][0] // 2)
 
         def late_pair(stage, n, lag):
-            for extra in sorted(set([0] + list({}.values())), reverse=True):
+            for extra in sorted(set([0] + list({7: 3}.values())), reverse=True):
                 c = n - lag - extra
-                if closes(c) and {}.get(STEPS[c][0], 0) == extra:
+                if closes(c) and {7: 3}.get(STEPS[c][0], 0) == extra:
                     run_pair(stage, c)
 
         def late_close(stage, n, lag):
-            for extra in sorted(set([0] + list({}.values())), reverse=True):
+            for extra in sorted(set([0] + list({7: 3}.values())), reverse=True):
                 c = n - lag - extra
-                if closes(c) and {}.get(STEPS[c][0], 0) == extra:
+                if closes(c) and {7: 3}.get(STEPS[c][0], 0) == extra:
                     run_close(stage, c)
+
+        def run_early(stage, n, lead, more):
+            for m in (n + lead, n + lead + 1):
+                if 0 <= m < len(STEPS):
+                    extra = 1 if STEPS[m] in more else 0
+                    if m - n == lead + extra:
+                        stage(m)
 
         def warm_up():
             bank = ps_o.tile([P, P], F32, name="warm_bank", tag="o_bank")
-            for index in range(16):
+            for index in range(14):
                 nc.tensor.matmul(
                     out=bank[:], lhsT=ones[:], rhs=ones[:], start=True, stop=True
                 )
@@ -635,7 +651,7 @@ def tile_refphi4flashdiffattention_pa_kernel(
         def tick(n):
             run(exponent, n)
             run(regroup, n - 1, closing=True)
-            run(row_tops, n + 1)
+            run_early(row_tops, n, 1, ())
             if False:
                 run_close(invert_sums, n - 1)
             if not False:
@@ -643,17 +659,17 @@ def tile_refphi4flashdiffattention_pa_kernel(
             run(quantise, n - 2, closing=True)
             quantised = closes(n - 2)
             if quantised or True:
-                run(shift, n + 1)
+                run_early(shift, n, 1, ())
             if True:
                 run_close(invert_sums, n - 1)
-            run_pair(lambda i, p: scale_first(i, p) if i in () else None, n - 3)
+            run_pair(lambda i, p: scale_first(i, p) if i in (2,) else None, n - 3)
             run_pair(combine, n - 3)
             if not (quantised or True):
                 run(shift, n + 1)
             run_close(weigh, n - 1)
             late_pair(lambda i, p: measure(i, p) if i in () else None, n, 4)
             late_pair(lambda i, p: finish(i, p) if i not in () else None, n, 6)
-            run_pair(lambda i, p: scale_first(i, p) if i not in () else None, n - 2)
+            run_pair(lambda i, p: scale_first(i, p) if i not in (2,) else None, n - 2)
             late_pair(lambda i, p: measure(i, p) if i not in () else None, n, 4)
             if False:
                 run_close(add_sums, n - 1)
@@ -662,7 +678,7 @@ def tile_refphi4flashdiffattention_pa_kernel(
             run_pair(lambda i, p: finish(i, p) if i in () else None, n - 5)
             for group in ROWS.get(n - 1, ()):
                 copy_rows(group[0])
-            run(scores, n + 2)
+            run_early(scores, n, 2, ((3, (1,)), (3, (2,)), (3, (3,))))
             run(turn, n, closing=True)
             run(attend, n - 2, closing=True)
             for group in ROWS.get(n, ()):
@@ -677,7 +693,7 @@ def tile_refphi4flashdiffattention_pa_kernel(
         for nm, tk in [('c24',-6),('spread',1),('prod',2),('gain',2),('rv0',3),('rv1',4),('dots',4),('signs',5),('qv0',4),('p2',4),('p1',4),('p0',4),('qv1',5),('p4',5),('p5',5),('p6',5)]:
             ONCE.setdefault(tk, []).append(fns[nm])
 
-        if 16:
+        if 14:
             warm_up()
         for n in range(-6, len(STEPS) + 6 + 12):
             tick(n)

@@ -461,6 +461,11 @@ def tile_refphi4flashdiffattention_pa_kernel(
         def attend(n):
             i, (h,) = STEPS[n]
             bank = ps_o.tile([P, 2, PAIR_DIM], F32, name="o_bank")
+            if not shares(i):
+                for index in range({7: 2, 3: 2}.get(i, 0)):
+                    nc.tensor.matmul(
+                        out=bank[:, 1, 0:P], lhsT=ones[:], rhs=ones[:], start=True, stop=True
+                    )
             features = slice(h // 2 * PAIR_DIM, (h // 2 + 1) * PAIR_DIM)
             passes = [(0, v_codes[0], v_scales[0])]
             if i == 7:
@@ -683,6 +688,12 @@ def tile_refphi4flashdiffattention_pa_kernel(
             run(attend, n - 2, closing=True)
             for group in ROWS.get(n, ()):
                 turn_rows(group[0])
+            if n in {4: 4, 5: 4}:
+                bank = ps_o.tile([P, P], F32, name="warm_bank", tag="o_bank")
+                for index in range({4: 4, 5: 4}[n]):
+                    nc.tensor.matmul(
+                        out=bank[:], lhsT=ones[:], rhs=ones[:], start=True, stop=True
+                    )
             for once in ONCE.get(n, []):
                 once()
 

import math
from contextlib import ExitStack

import concourse.mybir as mybir
from concourse.masks import make_identity

BF16 = mybir.dt.bfloat16
F32 = mybir.dt.float32
I32 = mybir.dt.int32
U32 = mybir.dt.uint32
U8 = mybir.dt.uint8
FP8X4 = mybir.dt.float8_e4m3fn_x4
ALU = mybir.AluOpType
FUNC = mybir.ActivationFunctionType
AXIS = mybir.AxisListType

P = 128
SEQ = 1024
HEADS = 4
PAIRS = HEADS // 2
DIM = 128
ROW = HEADS * DIM
PAIR_DIM = 2 * DIM
PACK = 4
K_PASS = P * PACK
TILES_PER_PASS = K_PASS // P
TILE_PARTS = P // TILES_PER_PASS
PASSES = SEQ // K_PASS
Q_TILES = SEQ // P

SCALE = 1.0 / math.sqrt(DIM)
LAMBDA_INIT = 0.8 - 0.6 * math.exp(-0.3 * 12)
NEG_INF = -1e30
EPS = 1e-5
X_TILES = 16

TILE_ORDER = (0, 1, 2, 4, 5, 6, 7, 3)
TOGETHER = {0: 4, 1: 2, 2: 2}
STEPS = [
    (i, tuple(range(h, h + TOGETHER.get(i, 1))))
    for i in TILE_ORDER
    for h in range(0, HEADS, TOGETHER.get(i, 1))
]

FLOPS = 2 * HEADS * (512 * 512 + 512 * 1024) * (DIM + PAIR_DIM)


def key_order(columns, ordered):
    pattern = "q (u p e) -> q u p e" if ordered else "q (p u e) -> q u p e"
    return columns.rearrange(pattern, u=2, e=2)


def partner(i):
    return 6 - i


def shares(i):
    return i in (4, 5, 6)


def passes_of(i):
    return 0 if i < 3 else 1 if i == 3 else 2


def segments(i):
    if i < TILES_PER_PASS:
        owner, number = (3, 0) if i == 3 else (partner(i), 1)
        return [(0, 0, (i + 1) * P, i * P, owner, number)]
    width = (i - TILES_PER_PASS + 1) * P
    return [(0, 0, K_PASS, None, i, 0), (1, K_PASS - width, width, 0, i, 1)]


def tile_refphi4flashdiffattention_pa_kernel(
    tc, q, k, v, lambda_q1, lambda_k1, lambda_q2, lambda_k2, subln_weight, out
):
    nc = tc.nc

    q_rows = q.rearrange("b (j p) h d -> p (b j) (h d)", p=P)
    k_rows = k.rearrange("b (j p) h d -> p (b j) (h d)", p=P)
    out_rows = out.rearrange("b (j p) h d -> p (b j) (h d)", p=P)
    v_pass_rows = v.rearrange("b (g p t) h d -> p (b g) (t h d)", p=P, t=PACK)
    v_tile_rows = v.rearrange("b (j p t) h d -> p (b j) (t h d)", p=TILE_PARTS, t=PACK)

    with ExitStack() as stack:
        keep = stack.enter_context(tc.tile_pool(name="keep", bufs=1))
        work = stack.enter_context(tc.tile_pool(name="work", bufs=6))
        small = stack.enter_context(tc.tile_pool(name="small", bufs=6))
        ps_s = stack.enter_context(tc.psum_pool(name="ps_s", bufs=4))
        ps_t = stack.enter_context(tc.psum_pool(name="ps_t", bufs=2))
        ps_o = stack.enter_context(tc.psum_pool(name="ps_o", bufs=2))

        stack.enter_context(tc.manual_schedule())

        ones = keep.tile([P, P], BF16, name="ones")
        nc.vector.memset(ones[:], 1.0)
        zero = keep.tile([P, X_TILES], F32, name="zero")
        nc.vector.memset(zero[:], 0.0)
        first_row = keep.tile([P, 4 * DIM + PAIR_DIM], BF16, name="first_row")
        nc.vector.memset(first_row[:].bitcast(U32), 0)

        exp_one = keep.tile([P, 1], F32, name="exp_one")
        nc.scalar.activation(out=exp_one[:], in_=zero[:, 0:1], func=FUNC.Exp)

        q_sb = {}
        k_sb = {}
        v_raw = [keep.tile([P, PACK, ROW], BF16, name="v_raw%d" % g) for g in range(PASSES)]

        def load_rows(first, last):
            for rows, tiles, name in ((k_rows, k_sb, "k"), (q_rows, q_sb, "q")):
                tile = keep.tile([P, last - first, ROW], BF16, name="%s_sb%d" % (name, first))
                nc.sync.dma_start(out=tile[:], in_=rows[:, first:last, :])
                for j in range(first, last):
                    tiles[j] = tile[:, j - first, :]

        for first, last in ((0, 1), (1, 2), (2, 3), (3, 5)):
            load_rows(first, last)
        for slot, vector in enumerate((lambda_q1, lambda_q2, lambda_k1, lambda_k2)):
            nc.sync.dma_start(
                out=first_row[0:1, slot * DIM : (slot + 1) * DIM], in_=vector.unsqueeze(0)
            )
        nc.sync.dma_start(out=first_row[0:1, 4 * DIM :], in_=subln_weight.unsqueeze(0))
        nc.sync.dma_start(out=v_raw[0][:].rearrange("p t c -> p (t c)"), in_=v_pass_rows[:, 0, :])
        for b in range(TILES_PER_PASS):
            nc.sync.dma_start(
                out=v_raw[1][b * TILE_PARTS : (b + 1) * TILE_PARTS, :, :].rearrange(
                    "p t c -> p (t c)"
                ),
                in_=v_tile_rows[:, Q_TILES - 1 - b, :],
            )
        load_rows(5, 8)

        ident_bf = keep.tile([P, P], BF16, name="ident_bf")
        make_identity(nc, ident_bf[:])
        mask_f32 = keep.tile([P, P], F32, name="mask_f32")
        nc.gpsimd.memset(mask_f32[:], 0.0)
        nc.gpsimd.affine_select(
            out=mask_f32[:],
            in_=mask_f32[:],
            pattern=[[-1, P]],
            compare_op=ALU.is_ge,
            fill=NEG_INF,
            base=0,
            channel_multiplier=1,
        )
        mask_bf = keep.tile([P, P], BF16, name="mask_bf")
        nc.vector.tensor_copy(out=key_order(mask_bf[:], True), in_=key_order(mask_f32[:], False))
        order_bf = keep.tile([P, P], BF16, name="order_bf")
        nc.vector.tensor_copy(out=key_order(order_bf[:], True), in_=key_order(ident_bf[:], False))
        ident_f32 = keep.tile([P, P], F32, name="ident_f32")
        make_identity(nc, ident_f32[:])
        minus_half = keep.tile([P, 2], F32, name="minus_half")
        nc.gpsimd.memset(minus_half[:], -0.5)

        x_all = keep.tile([P, X_TILES, PAIR_DIM + 1], F32, name="x_all")
        nc.vector.tensor_scalar(
            out=x_all[:, :, PAIR_DIM],
            in0=zero[:],
            scalar1=0.0,
            scalar2=math.sqrt(PAIR_DIM * EPS),
            op0=ALU.mult,
            op1=ALU.add,
        )
        x_tiles = [x_all[:, index, :] for index in range(X_TILES)]

        lam_in = keep.tile([P, 2, DIM], F32, name="lam_in")
        products = keep.tile([P, 2, DIM], F32, name="products")
        unread = keep.tile([P, 2, DIM], F32, name="unread")
        dots = keep.tile([P, 2], F32, name="dots")
        powers = keep.tile([P, 2], F32, name="powers")
        minus_lam = keep.tile([P, 1], F32, name="minus_lam")
        gain = keep.tile([P, PAIR_DIM], F32, name="gain")
        spread_banks = {}

        def spread_vectors():
            lam_bank = ps_o.tile([P, 4, DIM], F32, name="lam_bank", tag="o_bank")
            nc.tensor.matmul(
                out=lam_bank[:].rearrange("p s d -> p (s d)"),
                lhsT=ones[:],
                rhs=first_row[:, 0 : 4 * DIM],
                start=True,
                stop=True,
            )
            weight_bank = ps_o.tile([P, PAIR_DIM], F32, name="weight_bank", tag="o_bank")
            nc.tensor.matmul(
                out=weight_bank[:], lhsT=ones[:], rhs=first_row[:, 4 * DIM :], start=True, stop=True
            )
            spread_banks["lam"] = lam_bank
            spread_banks["weight"] = weight_bank

        def lam_products():
            bank = spread_banks["lam"]
            nc.scalar.copy(out=lam_in[:], in_=bank[:, 2:4, :])
            nc.vector.tensor_tensor(
                out=products[:], in0=bank[:, 0:2, :], in1=lam_in[:], op=ALU.mult
            )

        def scale_gain():
            nc.scalar.mul(
                out=gain[:],
                in_=spread_banks["weight"][:],
                mul=(1.0 - LAMBDA_INIT) * math.sqrt(PAIR_DIM),
            )

        def lam_dots():
            for term in range(2):
                nc.scalar.activation(
                    out=unread[:, term, :],
                    in_=products[:, term, :],
                    func=FUNC.Copy,
                    accum_out=dots[:, term : term + 1],
                )

        def lam_signs():
            nc.scalar.activation(out=powers[:], in_=dots[:], func=FUNC.Exp)
            nc.vector.tensor_scalar(
                out=minus_lam[:],
                in0=powers[:, 1:2],
                scalar1=powers[:, 0:1],
                scalar2=LAMBDA_INIT,
                op0=ALU.subtract,
                op1=ALU.subtract,
            )

        v_grouped = [
            keep.tile([P, ROW * PACK], BF16, name="v_grouped%d" % g, align_bytes=64)
            for g in range(PASSES)
        ]
        v_codes = [
            keep.tile([P, ROW], U32, name="v_codes%d" % g, align_bytes=64) for g in range(PASSES)
        ]
        v_scales = [
            keep.tile([P, ROW], U8, name="v_scales%d" % g, align_bytes=64) for g in range(PASSES)
        ]
        v_part = {}
        for i in (2, 4, 1, 5, 0, 6):
            v_part[i] = keep.tile([P, ROW], U32, name="v_part%d" % i, align_bytes=64)

        no_codes = keep.tile([P, ROW], U32, name="no_codes", align_bytes=64)
        nc.vector.memset(no_codes[:], 0)

        def part_rows(i):
            own = (i + 1) * TILE_PARTS if i < TILES_PER_PASS else (Q_TILES - 1 - i) * TILE_PARTS
            return (slice(0, own), slice(own, P)) if i < TILES_PER_PASS else (slice(own, P), slice(0, own))

        def clear_part(i):
            rest = part_rows(i)[1]
            nc.sync.dma_start(
                out=v_part[i][rest, :].bitcast(I32), in_=no_codes[rest, :].bitcast(I32)
            )

        def regroup_values(g):
            w = 160
            if w < ROW:
              nc.vector.tensor_copy(
                out=v_grouped[g][:,0:(ROW-w)*4].rearrange("p (c i t) -> p c t i", i=4, t=PACK),
                in_=v_raw[g][:,:,0:ROW-w].rearrange("p t (c i) -> p c t i", i=4),
              )
            if w:
              nc.scalar.copy(
                out=v_grouped[g][:,(ROW-w)*4:].rearrange("p (c i t) -> p c t i", i=4, t=PACK),
                in_=v_raw[g][:,:,ROW-w:].rearrange("p t (c i) -> p c t i", i=4),
              )

        def quantise_values(g):
            nc.vector.quantize_mx(
                out=v_codes[g][:].bitcast(FP8X4), scales=v_scales[g][:], in_=v_grouped[g][:]
            )

        def part_values(i):
            g = i // TILES_PER_PASS
            first = 0 if g == 0 else (Q_TILES - 1 - i) * TILE_PARTS
            last = (i + 1) * TILE_PARTS if g == 0 else P
            nc.sync.dma_start(
                out=v_part[i][first:last, :].bitcast(I32), in_=v_codes[g][first:last, :].bitcast(I32)
            )

        turned = keep.tile([P, Q_TILES, 2, HEADS, P], BF16, name="turned")

        def slot(j):
            return j if j < TILES_PER_PASS else 3 * TILES_PER_PASS - 1 - j

        rows_ps = {}

        def turn_rows(j):
            pool, tag = (ps_o, "o_bank") if j in (1, 3) else (ps_t, "t")
            banks = []
            for which, rows, order in ((0, k_sb, order_bf), (1, q_sb, ident_bf)):
                if which == 0 or j in (0,):
                    banks.append(pool.tile([P, 2, HEADS, P], BF16, name="rows_bank", tag=tag))
                for h in range(HEADS):
                    nc.tensor.transpose(
                        banks[-1][:, which, h, :], rows[j][:, h * DIM : (h + 1) * DIM], order[:]
                    )
            rows_ps[j] = banks

        def copy_rows(j):
            banks = rows_ps[j]
            if len(banks) == 2:
                for which, bank in enumerate(banks):
                    nc.vector.tensor_copy(
                        out=turned[:, slot(j), which, :, :], in_=bank[:, which, :, :]
                    )
            else:
                nc.vector.tensor_copy(out=turned[:, slot(j), :, :, :], in_=banks[0][:])

        e_tiles = {}
        for i in (4, 5, 6, 7, 3):
            for h in range(HEADS):
                e_tiles[i, h] = keep.tile(
                    [P, passes_of(i), 2, K_PASS // 2], BF16, name="e_tile%d_%d" % (i, h)
                )
        s_banks = {}
        tops = {}
        shifts = {}
        totals = {}
        partial_sums = {}
        inverses = {}
        factors = {}
        for i in (4, 5, 6, 7, 3):
            for pair in range(PAIRS):
                columns = 4 if shares(i) else 2
                suffix = "%d_%d" % (i, pair)
                totals[i, pair] = keep.tile([P, columns], F32, name="totals" + suffix)
                inverses[i, pair] = keep.tile([P, columns], F32, name="inverses" + suffix)
                factors[i, pair] = keep.tile([P, columns // 2], F32, name="factors" + suffix)
                if len(segments(i)) == 2:
                    partial_sums[i, pair] = keep.tile([P, 2, 2], F32, name="partial" + suffix)
        e_banks = {}
        e_grouped = {}
        e_codes = {}
        e_scales = {}
        o_banks = {}

        def scores(n):
            i, heads = STEPS[n]
            pieces = []
            bank = None
            column = K_PASS
            for h in heads:
                for s, (g, first, width, diagonal, owner, number) in enumerate(segments(i)):
                    if column + width > K_PASS:
                        bank = ps_s.tile([P, K_PASS], F32, name="s_bank")
                        column = 0
                    nc.tensor.matmul(
                        out=bank[:, column : column + width].rearrange("q (j c) -> q j c", c=P),
                        lhsT=turned[:, slot(i), 1, h, :],
                        rhs=turned[
                            :, (g * K_PASS + first) // P : (g * K_PASS + first + width) // P, 0, h, :
                        ],
                        start=True,
                        stop=diagonal is None,
                    )
                    if diagonal is not None:
                        nc.tensor.matmul(
                            out=bank[:, column + diagonal : column + diagonal + P],
                            lhsT=ident_bf[:],
                            rhs=mask_bf[:],
                            start=False,
                            stop=True,
                        )
                    pieces.append((bank, column, h, s))
                    column += width
            s_banks[n] = pieces

        def row_tops(n):
            i, heads = STEPS[n]
            top = small.tile([P, HEADS], F32, name="top")
            pieces = s_banks[n]
            index = 0
            while index < len(pieces):
                bank, column, h, s = pieces[index]
                width = segments(i)[s][2]
                count = sum(1 for piece in pieces if piece[0] is bank)
                nc.vector.tensor_reduce(
                    out=top[:, index : index + count],
                    in_=bank[:, 0 : count * width].rearrange("p (c w) -> p c w", c=count),
                    axis=AXIS.X,
                    op=ALU.max,
                )
                index += count
            tops[n] = top

        def shift(n):
            i, heads = STEPS[n]
            bias = small.tile([P, HEADS], F32, name="bias")
            if len(segments(i)) == 2:
                (nc.gpsimd if i in (0, 1, 2, 3, 4, 5, 6, 7) else nc.vector).tensor_scalar(
                    out=bias[:, 0:1],
                    in0=tops[n][:, 0:1],
                    scalar1=tops[n][:, 1:2],
                    scalar2=-SCALE,
                    op0=ALU.max,
                    op1=ALU.mult,
                )
            else:
                if i in (0, 1, 2, 3, 4, 5, 6, 7):
                    nc.gpsimd.tensor_scalar(
                        out=bias[:, 0 : len(heads)], in0=tops[n][:, 0 : len(heads)],
                        scalar1=-SCALE, scalar2=0.0, op0=ALU.mult, op1=ALU.add,
                    )
                else:
                    nc.vector.tensor_scalar_mul(
                        out=bias[:, 0 : len(heads)], in0=tops[n][:, 0 : len(heads)], scalar1=-SCALE
                    )
            shifts[n] = bias

        def exponent(n):
            i, heads = STEPS[n]
            parts = segments(i)
            for bank, column, h, s in s_banks[n]:
                pair, half = divmod(h, 2)
                g, first, width, diagonal, owner, number = parts[s]
                if len(parts) == 2:
                    row_sum = partial_sums[i, pair][:, half, s : s + 1]
                else:
                    column_of_sum = half if i == owner else 2 + half
                    row_sum = totals[owner, pair][:, column_of_sum : column_of_sum + 1]
                index = h - heads[0]
                nc.scalar.activation(
                    out=e_tiles[owner, h][
                        :, number, :, first // 2 : (first + width) // 2
                    ].rearrange("q u (j w) -> q u j w", w=P // 2),
                    in_=bank[:, column : column + width].rearrange(
                        "q (j u w) -> q u j w", u=2, w=P // 2
                    ),
                    func=FUNC.Exp,
                    bias=shifts[n][:, index : index + 1],
                    scale=SCALE,
                    accum_out=row_sum,
                )

        def turn(n):
            i, (h,) = STEPS[n]
            bank = ps_t.tile([P, passes_of(i), 2, P], F32, name="e_bank", tag="t")
            for number in range(passes_of(i)):
                for u in range(2):
                    nc.tensor.transpose(
                        bank[:, number, u, :],
                        e_tiles[i, h][:, number, u, :].bitcast(F32),
                        ident_f32[:],
                    )
            e_banks[n] = bank

        def regroup(n):
            passes = passes_of(STEPS[n][0])
            grouped = work.tile([P, passes * K_PASS], BF16, name="grouped", align_bytes=64)
            nc.scalar.copy(
                out=grouped[:].bitcast(F32).rearrange("p (g r u) -> p g r u", g=passes, u=2),
                in_=e_banks[n][:].rearrange("p g u r -> p g r u"),
            )
            e_grouped[n] = grouped

        def quantise(n):
            passes = passes_of(STEPS[n][0])
            codes = work.tile([P, passes * P], U32, name="codes", align_bytes=64)
            scales = work.tile([P, passes * P], U8, name="scales", align_bytes=64)
            nc.vector.quantize_mx(out=codes[:].bitcast(FP8X4), scales=scales[:], in_=e_grouped[n][:])
            e_codes[n] = codes
            e_scales[n] = scales

        def attend(n):
            i, (h,) = STEPS[n]
            bank = ps_o.tile([P, 2, PAIR_DIM], F32, name="o_bank")
            if not shares(i):
                for index in range({7: 2, 3: 2}.get(i, 0)):
                    nc.tensor.matmul(
                        out=bank[:, 1, 0:P], lhsT=ones[:], rhs=ones[:], start=True, stop=True
                    )
            features = slice(h // 2 * PAIR_DIM, (h // 2 + 1) * PAIR_DIM)
            passes = [(0, v_codes[0], v_scales[0])]
            if i == 7:
                passes.append((1, v_codes[1], v_scales[1]))
            if shares(i):
                passes.append((1, v_part[i], v_scales[1]))
            products = [passes]
            if shares(i):
                products.append([(1, v_part[partner(i)], v_scales[0])])
            for place, passes in enumerate(products):
                for index, (number, codes, scales) in enumerate(passes):
                    queries = slice(number * P, (number + 1) * P)
                    nc.tensor.matmul_mx(
                        out=bank[:, place, :],
                        lhsT=e_codes[n][:, queries].bitcast(FP8X4),
                        lhsT_scale=e_scales[n][:, queries],
                        rhs=codes[:, features].bitcast(FP8X4),
                        rhs_scale=scales[:, features],
                        start=(index == 0),
                        stop=(index == len(passes) - 1),
                    )
            o_banks[i, h] = bank

        firsts = {}
        xs = {}
        sums_sq = {}
        rstds = {}

        def side(i):
            return (partner(i), 1) if i < 3 else (i, 0)

        def add_sums(i, pair):
            if len(segments(i)) == 2:
                parts = partial_sums[i, pair]
                if False:
                    nc.gpsimd.tensor_tensor(
                        out=totals[i, pair][:, 0:2], in0=parts[:, :, 0], in1=parts[:, :, 1], op=ALU.add
                    )
                else:
                    nc.vector.tensor_reduce(
                        out=totals[i, pair][:, 0:2], in_=parts[:], axis=AXIS.X, op=ALU.add
                    )

        def invert_sums(i, pair):
            nc.vector.reciprocal(out=inverses[i, pair][:], in_=totals[i, pair][:])

        def weigh(i, pair):
            nc.vector.tensor_scalar_mul(
                out=factors[i, pair][:],
                in0=inverses[i, pair][:].rearrange("p (t h) -> p t h", h=2)[:, :, 1],
                scalar1=minus_lam[:, 0:1],
            )

        def scale_first(i, pair):
            owner, place = side(i)
            scaled = work.tile([P, PAIR_DIM], F32, name="scaled")
            if i in (2,):
                nc.vector.tensor_scalar_mul(
                    out=scaled[:],
                    in0=o_banks[owner, 2 * pair][:, place, :],
                    scalar1=inverses[owner, pair][:, 2 * place : 2 * place + 1],
                )
            else:
                nc.scalar.activation(
                    out=scaled[:],
                    in_=o_banks[owner, 2 * pair][:, place, :],
                    func=FUNC.Copy,
                    scale=inverses[owner, pair][:, 2 * place : 2 * place + 1],
                )
            firsts[i, pair] = scaled

        def combine(i, pair):
            owner, place = side(i)
            x = x_tiles[len(xs) % X_TILES]
            nc.vector.scalar_tensor_tensor(
                out=x[:, 0:PAIR_DIM],
                in0=o_banks[owner, 2 * pair + 1][:, place, :],
                scalar=factors[owner, pair][:, place : place + 1],
                in1=firsts[i, pair][:],
                op0=ALU.mult,
                op1=ALU.add,
            )
            xs[i, pair] = x

        def measure(i, pair):
            owner, place = side(i)
            if (owner, pair) not in sums_sq:
                sums_sq[owner, pair] = small.tile([P, 2], F32, name="sum_sq")
            squares = work.tile([P, PAIR_DIM + 1], F32, name="squares")
            sum_sq = sums_sq[owner, pair][:, place : place + 1]
            x = xs[i, pair]
            if i in ():
                nc.vector.scalar_tensor_tensor(
                    out=squares[:], in0=x, scalar=1.0, in1=x, op0=ALU.mult, op1=ALU.mult,
                    accum_out=sum_sq,
                )
            else:
                nc.scalar.activation(out=squares[:], in_=x, func=FUNC.Square, accum_out=sum_sq)

        def root(i, pair):
            count = 2 if shares(i) else 1
            rstd = small.tile([P, 2], F32, name="rstd")
            nc.gpsimd.tensor_tensor(
                out=rstd[:, 0:count],
                in0=sums_sq[i, pair][:, 0:count],
                in1=minus_half[:, 0:count],
                op=ALU.pow,
            )
            rstds[i, pair] = rstd

        gained = {}

        def apply_gain(i, pair):
            product = work.tile([P, PAIR_DIM], F32, name="product")
            nc.gpsimd.tensor_tensor(
                out=product[:], in0=xs[i, pair][:, 0:PAIR_DIM], in1=gain[:], op=ALU.mult
            )
            gained[i, pair] = product

        def finish(i, pair):
            owner, place = side(i)
            y = work.tile([P, PAIR_DIM], F32, name="y")
            rstd = rstds[owner, pair][:, place : place + 1]
            if i in ():
                nc.gpsimd.tensor_scalar(
                    out=y[:], in0=gained[i, pair][:], scalar1=rstd, scalar2=1.0,
                    op0=ALU.mult, op1=ALU.mult,
                )
            else:
                nc.vector.scalar_tensor_tensor(
                    out=y[:],
                    in0=xs[i, pair][:, 0:PAIR_DIM],
                    scalar=rstd,
                    in1=gain[:],
                    op0=ALU.mult,
                    op1=ALU.mult,
                )
            nc.sync.dma_start(
                out=out_rows[:, i, pair * PAIR_DIM : (pair + 1) * PAIR_DIM], in_=y[:]
            )

        def closes(n):
            return 0 <= n < len(STEPS) and passes_of(STEPS[n][0]) > 0

        def run(stage, n, closing=False):
            if 0 <= n < len(STEPS) and (not closing or closes(n)):
                stage(n)

        def run_pair(stage, c):
            if closes(c) and STEPS[c][1][0] % 2 == 1:
                i, (h,) = STEPS[c]
                stage(i, h // 2)
                if shares(i):
                    stage(partner(i), h // 2)

        def run_close(stage, c):
            if closes(c) and STEPS[c][1][0] % 2 == 1:
                stage(STEPS[c][0], STEPS[c][1][0] // 2)

        def late_pair(stage, n, lag):
            for extra in sorted(set([0] + list({7: 3}.values())), reverse=True):
                c = n - lag - extra
                if closes(c) and {7: 3}.get(STEPS[c][0], 0) == extra:
                    run_pair(stage, c)

        def late_close(stage, n, lag):
            for extra in sorted(set([0] + list({7: 3}.values())), reverse=True):
                c = n - lag - extra
                if closes(c) and {7: 3}.get(STEPS[c][0], 0) == extra:
                    run_close(stage, c)

        def run_early(stage, n, lead, more):
            for m in (n + lead, n + lead + 1):
                if 0 <= m < len(STEPS):
                    extra = 1 if STEPS[m] in more else 0
                    if m - n == lead + extra:
                        stage(m)

        def warm_up():
            bank = ps_o.tile([P, P], F32, name="warm_bank", tag="o_bank")
            for index in range(14):
                nc.tensor.matmul(
                    out=bank[:], lhsT=ones[:], rhs=ones[:], start=True, stop=True
                )

        ROWS = {-4: ((0, 1),), -3: ((1, 2),), -1: ((2, 3),), 0: ((3, 4),), 1: ((4, 5),), 5: ((5, 6),), 9: ((6, 7),), 13: ((7, 8),)}

        def tick(n):
            run(exponent, n)
            run(regroup, n - 1, closing=True)
            run_early(row_tops, n, 1, ())
            if False:
                run_close(invert_sums, n - 1)
            if not False:
                run_close(add_sums, n - 1)
            run(quantise, n - 2, closing=True)
            quantised = closes(n - 2)
            if quantised or True:
                run_early(shift, n, 1, ())
            if True:
                run_close(invert_sums, n - 1)
            run_pair(lambda i, p: scale_first(i, p) if i in (2,) else None, n - 3)
            run_pair(combine, n - 3)
            if not (quantised or True):
                run(shift, n + 1)
            run_close(weigh, n - 1)
            late_pair(lambda i, p: measure(i, p) if i in () else None, n, 4)
            late_pair(lambda i, p: finish(i, p) if i not in () else None, n, 6)
            run_pair(lambda i, p: scale_first(i, p) if i not in (2,) else None, n - 2)
            late_pair(lambda i, p: measure(i, p) if i not in () else None, n, 4)
            if False:
                run_close(add_sums, n - 1)
            late_close(root, n, 4)
            run_pair(lambda i, p: apply_gain(i, p) if i in () else None, n - 4)
            run_pair(lambda i, p: finish(i, p) if i in () else None, n - 5)
            for group in ROWS.get(n - 1, ()):
                copy_rows(group[0])
            run_early(scores, n, 2, ((3, (1,)), (3, (2,)), (3, (3,))))
            run(turn, n, closing=True)
            run(attend, n - 2, closing=True)
            for group in ROWS.get(n, ()):
                turn_rows(group[0])
            if n in {4: 4, 5: 4}:
                bank = ps_o.tile([P, P], F32, name="warm_bank", tag="o_bank")
                for index in range({4: 4, 5: 4}[n]):
                    nc.tensor.matmul(
                        out=bank[:], lhsT=ones[:], rhs=ones[:], start=True, stop=True
                    )
            for once in ONCE.get(n, []):
                once()

        ONCE = {}
        fns = dict(spread=spread_vectors, prod=lam_products, gain=scale_gain, dots=lam_dots, signs=lam_signs,
            rv0=lambda: regroup_values(0), rv1=lambda: regroup_values(1), qv0=lambda: quantise_values(0), qv1=lambda: quantise_values(1),
            p0=lambda: part_values(0), p1=lambda: part_values(1), p2=lambda: part_values(2), p4=lambda: part_values(4), p5=lambda: part_values(5), c24=lambda: [clear_part(i) for i in (2, 4, 1, 5, 0, 6)], p6=lambda: part_values(6))
        for nm, tk in [('c24',-6),('spread',1),('prod',2),('gain',2),('rv0',3),('rv1',4),('dots',4),('signs',5),('qv0',4),('p2',4),('p1',4),('p0',4),('qv1',5),('p4',5),('p5',5),('p6',5)]:
            ONCE.setdefault(tk, []).append(fns[nm])

        if 14:
            warm_up()
        for n in range(-6, len(STEPS) + 6 + 12):
            tick(n)
